import numpy as np
import ml_dtypes


def mxq(x, axis, fmt="e4m3"):
    dtype, down = {"e4m3": (ml_dtypes.float8_e4m3fn, 7), "e5m2": (ml_dtypes.float8_e5m2, 14)}[fmt]
    v = np.moveaxis(np.asarray(x, np.float32).astype(ml_dtypes.bfloat16).astype(np.float64), axis, -1)
    blocks = v.reshape(v.shape[:-1] + (-1, 32))
    amax = np.abs(blocks).max(-1, keepdims=True)
    byte = np.maximum(np.where(amax > 0, np.frexp(amax)[1] - 1 + 127, 0) - down, 1)
    scale = np.exp2(byte - 127.0)
    codes = (blocks / scale).astype(np.float32).astype(dtype).astype(np.float64)
    return np.moveaxis((codes * scale).reshape(v.shape), -1, axis)


WIDE = False


def mx_kscale(k):
    if not WIDE:
        return np.ones(k)
    levels = np.array([10, -10, 5, -5, 0])
    if k % 512:
        return np.exp2(np.random.permutation(np.resize(levels, k // 32))).repeat(32)
    a = np.empty((k // 512, 16))
    for p in range(k // 512):
        a[p, :8] = np.random.permutation(np.resize(levels, 8))
        for g in range(8):
            far = levels[np.abs(levels - a[p, g]) >= 10]
            a[p, g + 8] = far[np.random.randint(len(far))]
    return np.exp2(a.ravel()).repeat(32)


BF16 = ml_dtypes.bfloat16


def bf(x):
    return np.asarray(x, np.float32).astype(BF16)


def f64(x):
    return np.asarray(x).astype(np.float64)


B, N, D, L = 4, 1024, 512, 3
GAIN = 8.0


def setup_inputs():
    s, t = mx_kscale(N), mx_kscale(D)
    c = np.exp2(np.round(np.log2(np.mean(1.0 / s))))
    sc = s * c
    deg = np.exp2(np.random.uniform(-1.0, 2.0, (B, N, 1)))
    adj = deg * np.exp(2.0 * np.random.standard_normal((B, N, N)) - 2.0) / N
    return {"x": bf(np.random.standard_normal((B, N, D)) * sc[:, None] * t),
            "adj": bf(adj / sc),
            "w": bf(np.random.standard_normal((D, D)) * GAIN / np.sqrt(D) / t[:, None]),
            "b": bf(np.random.standard_normal(D) * 0.5)}


def reference(x, adj, w, b):
    a = f64(adj)
    denom = a.sum(axis=2, keepdims=True) + 1.0
    ax = mxq(a, 2, "e4m3") @ mxq(f64(x), 1, "e4m3")
    axw = (mxq(ax, 2, "e4m3") @ mxq(f64(w), 0, "e4m3")) + f64(b)
    return np.maximum(axw / denom, 0.0)

@@ -1,0 +1,293 @@
+from contextlib import ExitStack
+
+import concourse.mybir as mybir
+from concourse.masks import make_identity
+
+F32 = mybir.dt.float32
+BF16 = mybir.dt.bfloat16
+U32 = mybir.dt.uint32
+U8 = mybir.dt.uint8
+FP8X4 = mybir.dt.float8_e4m3fn_x4
+ALU = mybir.AluOpType
+ACT = mybir.ActivationFunctionType
+AX = mybir.AxisListType
+
+G = 4
+N = 1024
+D = 512
+P = 128
+R = N // P
+NU = G * R
+NPAIR = NU // 2
+FLOPS = 2 * G * N * N * D + 2 * G * N * D * D
+
+MANUAL = True
+C2_ON_V = tuple(range(1, NU, 3))
+B_ON_V = ()
+
+
+def tile_msamodel_pa_kernel(tc, x, adj, w, b, out):
+    nc = tc.nc
+    with ExitStack() as ctx:
+        const = ctx.enter_context(tc.tile_pool(name="const", bufs=1))
+        two = ctx.enter_context(tc.tile_pool(name="two", bufs=2))
+        four = ctx.enter_context(tc.tile_pool(name="four", bufs=6))
+        six = ctx.enter_context(tc.tile_pool(name="six", bufs=6))
+        ps_tp = ctx.enter_context(tc.psum_pool(name="ps_tp", bufs=2))
+        ps_p1 = ctx.enter_context(tc.psum_pool(name="ps_p1", bufs=3))
+        ps_p2 = ctx.enter_context(tc.psum_pool(name="ps_p2", bufs=2))
+        ps_pd = ctx.enter_context(tc.psum_pool(name="ps_pd", bufs=1))
+        if MANUAL:
+            ctx.enter_context(tc.manual_schedule())
+
+        adj_v = adj.rearrange("g (p r) j -> g p (r j)", r=R)
+        x_v = x.rearrange("g (c p t) d -> g p c (t d)", c=2, p=P, t=4)
+        out_v = out.rearrange("g (p r) e -> g p (r e)", r=R)
+
+        adj_sb = [const.tile([P, R * N], BF16, name="adj%d" % g) for g in range(G)]
+        adj_w = [t[:].bitcast(F32) for t in adj_sb]
+        x_sb = [const.tile([P, 4 * N], BF16, name="x%d" % g) for g in range(G)]
+        w_sb = const.tile([P, 4 * D], BF16, name="w_sb")
+        wg = const.tile([P, 4 * D], BF16, name="wg", align_bytes=64)
+        wc = const.tile([P, D], U32, name="wc", align_bytes=64)
+        ws = const.tile([P, D], U8, name="ws", align_bytes=64)
+        zb = const.tile([P, D], BF16, name="zb")
+        ones = const.tile([P, P], BF16, name="ones")
+        identf = const.tile([P, P], F32, name="identf")
+        bb = const.tile([P, D], F32, name="bb")
+        e_t = [const.tile([P, 4], F32, name="e_t%d" % k) for k in range(NU // 4)]
+        r_t = [const.tile([P, 4], F32, name="r_t%d" % k) for k in range(NU // 4)]
+
+        def load_adj(g, r0, r1):
+            nc.sync.dma_start(out=adj_sb[g][:, r0 * N : r1 * N], in_=adj_v[g, :, r0 * N : r1 * N])
+
+        def load_x(g, k0, k1):
+            nc.sync.dma_start(
+                out=x_sb[g][:, k0 * 2048 : k1 * 2048].rearrange("p (c f) -> p c f", f=2048),
+                in_=x_v[g, :, k0:k1, :],
+            )
+
+        load_x(0, 0, 1)
+        load_adj(0, 0, 1)
+        load_x(0, 1, 2)
+        load_adj(0, 1, 2)
+        load_adj(0, 2, 4)
+        nc.sync.dma_start(
+            out=w_sb[:],
+            in_=w.rearrange("(p t) e -> p (t e)", t=4),
+        )
+        load_adj(0, 4, 6)
+        load_x(1, 0, 2)
+        load_adj(0, 6, 8)
+        load_adj(1, 0, 4)
+        load_adj(1, 4, 8)
+        load_x(2, 0, 2)
+        load_adj(2, 0, 8)
+        load_x(3, 0, 2)
+        load_adj(3, 0, 8)
+
+        nc.vector.memset(zb[:], 0.0)
+        nc.vector.memset(ones[:], 1.0)
+        nc.scalar.dma_start(out=zb[0:1, :], in_=b.rearrange("(o n) -> o n", o=1))
+        make_identity(nc, identf[:])
+
+        st = {}
+
+        def regroup(dst, src):
+            nc.vector.tensor_copy(
+                out=dst.rearrange("p (c i t) -> p c t i", i=4, t=4),
+                in_=src.rearrange("p (t c i) -> p c t i", t=4, i=4),
+            )
+
+        def regroup_x(dst, src):
+            nc.vector.tensor_copy(
+                out=dst.rearrange("p (t m j) -> p t m j", t=4, j=4),
+                in_=src.rearrange("p (j m t) -> p t m j", t=4, j=4),
+            )
+
+        def xr(g, c):
+            if c == 0:
+                st["xg", g] = two.tile([P, 4 * N], BF16, name="xg%d" % g, tag="xg", align_bytes=64)
+            regroup_x(st["xg", g][:, c * 2048 : (c + 1) * 2048], x_sb[g][:, c * 2048 : (c + 1) * 2048])
+
+        def xq(g, c0, c1):
+            if c0 == 0:
+                st["xc", g] = two.tile([P, N], U32, name="xc%d" % g, tag="xc", align_bytes=64)
+                st["xs", g] = two.tile([P, N], U8, name="xs%d" % g, tag="xs", align_bytes=64)
+            nc.vector.quantize_mx(
+                out=st["xc", g][:, c0 * D : c1 * D].bitcast(FP8X4),
+                scales=st["xs", g][:, c0 * D : c1 * D],
+                in_=st["xg", g][:, c0 * 2048 : c1 * 2048],
+            )
+
+        def t_(n):
+            g, r = divmod(n, R)
+            tp = ps_tp.tile([P, 512], F32, name="tp%d" % n, tag="tp")
+            st["tp", n] = tp
+            for k in range(4):
+                nc.tensor.transpose(
+                    out=tp[:, k * P : (k + 1) * P],
+                    in_=adj_w[g][:, r * 512 + (k // 2) * 256 + k % 2 : r * 512 + (k // 2 + 1) * 256 : 2],
+                    identity=identf[:],
+                )
+
+        def a_(n):
+            gt = four.tile([P, N], BF16, name="gt%d" % n, tag="gt", align_bytes=64)
+            st["gt", n] = gt
+            nc.scalar.copy(
+                out=gt[:].bitcast(F32).rearrange("p (c i u) -> p c i u", c=2, u=2),
+                in_=st["tp", n][:].rearrange("p (c u i) -> p c i u", c=2, u=2),
+            )
+
+        def qa(n):
+            ac = four.tile([P, 256], U32, name="ac%d" % n, tag="ac", align_bytes=64)
+            sc = four.tile([P, 256], U8, name="as%d" % n, tag="as", align_bytes=64)
+            st["ac", n] = ac
+            st["as", n] = sc
+            nc.vector.quantize_mx(out=ac[:].bitcast(FP8X4), scales=sc[:], in_=st["gt", n][:])
+
+        def m1(n):
+            g = n // R
+            p1 = ps_p1.tile([P, 512], F32, name="p1_%d" % n, tag="p1")
+            st["p1", n] = p1
+            for t in range(4):
+                for c in range(2):
+                    lo = c * D + t * P
+                    nc.tensor.matmul_mx(
+                        out=p1[:, t * P : (t + 1) * P],
+                        lhsT=st["xc", g][:, lo : lo + P].bitcast(FP8X4),
+                        lhsT_scale=st["xs", g][:, lo : lo + P],
+                        rhs=st["ac", n][:, c * P : (c + 1) * P].bitcast(FP8X4),
+                        rhs_scale=st["as", n][:, c * P : (c + 1) * P],
+                        start=(c == 0),
+                        stop=(c == 1),
+                    )
+
+        def b_(n):
+            g2 = four.tile([P, D], BF16, name="g2_%d" % n, tag="g2", align_bytes=64)
+            st["g2", n] = g2
+            dst = g2[:].rearrange("p (i t) -> p i t", t=4)
+            src = st["p1", n][:].rearrange("p (t i) -> p i t", t=4)
+            if n in B_ON_V:
+                nc.vector.tensor_copy(out=dst, in_=src)
+            else:
+                nc.scalar.copy(out=dst, in_=src)
+
+        def qb(n):
+            c2 = four.tile([P, P], U32, name="bc%d" % n, tag="bc", align_bytes=64)
+            s2 = four.tile([P, P], U8, name="bs%d" % n, tag="bs", align_bytes=64)
+            st["bc", n] = c2
+            st["bs", n] = s2
+            nc.vector.quantize_mx(out=c2[:].bitcast(FP8X4), scales=s2[:], in_=st["g2", n][:])
+
+        def m2(n):
+            p2 = ps_p2.tile([P, D], F32, name="p2_%d" % n, tag="p2")
+            st["p2", n] = p2
+            nc.tensor.matmul_mx(
+                out=p2[:],
+                lhsT=st["bc", n][:].bitcast(FP8X4),
+                lhsT_scale=st["bs", n][:],
+                rhs=wc[:].bitcast(FP8X4),
+                rhs_scale=ws[:],
+                start=True,
+                stop=True,
+            )
+
+        def c1(n):
+            z = four.tile([P, D], F32, name="z%d" % n, tag="z")
+            st["z", n] = z
+            nc.vector.tensor_tensor(out=z[:], in0=st["p2", n][:], in1=bb[:], op=ALU.add)
+
+        def c2(n):
+            if ("o", n // 2) not in st:
+                st["o", n // 2] = six.tile([P, 2 * D], F32, name="o%d" % (n // 2), tag="o")
+            o = st["o", n // 2][:, (n % 2) * D : (n % 2 + 1) * D]
+            rd = r_t[n // 4][:, n % 4 : n % 4 + 1]
+            if n in C2_ON_V:
+                nc.vector.tensor_scalar(
+                    out=o, in0=st["z", n][:], scalar1=rd, scalar2=0.0, op0=ALU.mult, op1=ALU.max
+                )
+            else:
+                nc.scalar.activation(out=o, in_=st["z", n][:], func=ACT.Relu, scale=rd)
+
+        def store(m, u0, u1):
+            g, k = divmod(m, R // 2)
+            nc.sync.dma_start(
+                out=out_v[g, :, (2 * k + u0) * D : (2 * k + u1) * D], in_=st["o", m][:, u0 * D : u1 * D]
+            )
+
+        def dn(n):
+            if n % 4 == 0:
+                st["pd", n // 4] = ps_pd.tile([P, 4], F32, name="pd%d" % (n // 4), tag="pd")
+            cols = st["gt", n][:].rearrange("p (c i t) -> p c t i", c=2, t=4)
+            for k in range(8):
+                nc.tensor.matmul(
+                    out=st["pd", n // 4][:, n % 4 : n % 4 + 1],
+                    lhsT=cols[:, k // 4, k % 4, :],
+                    rhs=ones[:, 0:1],
+                    start=(k == 0),
+                    stop=(k == 7),
+                )
+
+        def rb(k):
+            nc.vector.tensor_scalar_add(out=e_t[k][:], in0=st["pd", k][:], scalar1=1.0)
+            nc.vector.reciprocal(out=r_t[k][:], in_=e_t[k][:])
+
+        def pair(m):
+            return [2 * m, 2 * m + 1] if 0 <= m < NPAIR else []
+
+        xr(0, 0)
+        xr(0, 1)
+        xq(0, 0, 1)
+        xq(0, 1, 2)
+
+        for s in range(-1, NPAIR + 3):
+            g, q = divmod(s, 4)
+            if s == 2:
+                nc.scalar.copy(out=bb[:], in_=st["pb"][:])
+            for n in pair(s):
+                a_(n)
+            for n in pair(s - 1):
+                dn(n)
+            if s == 1:
+                st["pb"] = ps_p2.tile([P, D], F32, name="pb", tag="p2")
+                nc.tensor.matmul(out=st["pb"][:], lhsT=ones[:], rhs=zb[:], start=True, stop=True)
+            for n in pair(s + 1):
+                t_(n)
+            for n in pair(s - 2):
+                m2(n)
+            for n in pair(s):
+                qa(n)
+            for n in pair(s - 1):
+                b_(n)
+            for n in pair(s):
+                m1(n)
+            if s == 0:
+                regroup(wg[:], w_sb[:])
+            if s >= 0 and g + 1 < G:
+                if q == 1:
+                    xr(g + 1, 0)
+                if q == 2:
+                    xr(g + 1, 1)
+                if q == 3:
+                    xq(g + 1, 0, 2)
+            if s == 1:
+                nc.vector.quantize_mx(out=wc[:].bitcast(FP8X4), scales=ws[:], in_=wg[:])
+            if 2 <= s <= NPAIR and s % 2 == 0:
+                rb((s - 2) // 2)
+            for n in pair(s - 3):
+                if n in C2_ON_V:
+                    c2(n)
+                    if s - 3 == NPAIR - 1:
+                        store(s - 3, n % 2, n % 2 + 1)
+            for n in pair(s - 1):
+                qb(n)
+            for n in pair(s - 2):
+                c1(n)
+            for n in pair(s - 3):
+                if n not in C2_ON_V:
+                    c2(n)
+                    if s - 3 == NPAIR - 1:
+                        store(s - 3, n % 2, n % 2 + 1)
+            if 0 <= s - 3 < NPAIR - 1:
+                store(s - 3, 0, 2)

@@ -21,24 +21,21 @@ NU = G * R
 NPAIR = NU // 2
 FLOPS = 2 * G * N * N * D + 2 * G * N * D * D
 
-MANUAL = True
-C2_ON_V = tuple(range(1, NU, 3))
-B_ON_V = ()
-
 
 def tile_msamodel_pa_kernel(tc, x, adj, w, b, out):
     nc = tc.nc
     with ExitStack() as ctx:
         const = ctx.enter_context(tc.tile_pool(name="const", bufs=1))
         two = ctx.enter_context(tc.tile_pool(name="two", bufs=2))
-        four = ctx.enter_context(tc.tile_pool(name="four", bufs=6))
-        six = ctx.enter_context(tc.tile_pool(name="six", bufs=6))
+        gts = ctx.enter_context(tc.tile_pool(name="gts", bufs=10))
+        acs = ctx.enter_context(tc.tile_pool(name="acs", bufs=8))
+        four = ctx.enter_context(tc.tile_pool(name="four", bufs=4))
+        six = ctx.enter_context(tc.tile_pool(name="six", bufs=5))
         ps_tp = ctx.enter_context(tc.psum_pool(name="ps_tp", bufs=2))
         ps_p1 = ctx.enter_context(tc.psum_pool(name="ps_p1", bufs=3))
         ps_p2 = ctx.enter_context(tc.psum_pool(name="ps_p2", bufs=2))
         ps_pd = ctx.enter_context(tc.psum_pool(name="ps_pd", bufs=1))
-        if MANUAL:
-            ctx.enter_context(tc.manual_schedule())
+        ctx.enter_context(tc.manual_schedule())
 
         adj_v = adj.rearrange("g (p r) j -> g p (r j)", r=R)
         x_v = x.rearrange("g (c p t) d -> g p c (t d)", c=2, p=P, t=4)
@@ -61,34 +58,34 @@ def tile_msamodel_pa_kernel(tc, x, adj, w, b, out):
         def load_adj(g, r0, r1):
             nc.sync.dma_start(out=adj_sb[g][:, r0 * N : r1 * N], in_=adj_v[g, :, r0 * N : r1 * N])
 
-        def load_x(g, k0, k1):
+        def load_x(g, c0, c1):
             nc.sync.dma_start(
-                out=x_sb[g][:, k0 * 2048 : k1 * 2048].rearrange("p (c f) -> p c f", f=2048),
-                in_=x_v[g, :, k0:k1, :],
+                out=x_sb[g][:, c0 * 2048 : c1 * 2048].rearrange("p (c f) -> p c f", f=2048),
+                in_=x_v[g, :, c0:c1, :],
             )
+
+        nc.vector.memset(zb[:], 0.0)
+        nc.scalar.dma_start(out=zb[0:1, :], in_=b.rearrange("(o n) -> o n", o=1))
 
         load_x(0, 0, 1)
         load_adj(0, 0, 1)
         load_x(0, 1, 2)
         load_adj(0, 1, 2)
         load_adj(0, 2, 4)
-        nc.sync.dma_start(
-            out=w_sb[:],
-            in_=w.rearrange("(p t) e -> p (t e)", t=4),
-        )
         load_adj(0, 4, 6)
-        load_x(1, 0, 2)
+        nc.sync.dma_start(out=w_sb[:], in_=w.rearrange("(p t) e -> p (t e)", t=4))
         load_adj(0, 6, 8)
-        load_adj(1, 0, 4)
+        load_adj(1, 0, 2)
+        load_x(1, 0, 1)
+        load_x(1, 1, 2)
+        load_adj(1, 2, 4)
         load_adj(1, 4, 8)
         load_x(2, 0, 2)
         load_adj(2, 0, 8)
         load_x(3, 0, 2)
         load_adj(3, 0, 8)
 
-        nc.vector.memset(zb[:], 0.0)
         nc.vector.memset(ones[:], 1.0)
-        nc.scalar.dma_start(out=zb[0:1, :], in_=b.rearrange("(o n) -> o n", o=1))
         make_identity(nc, identf[:])
 
         st = {}
@@ -125,14 +122,15 @@ def tile_msamodel_pa_kernel(tc, x, adj, w, b, out):
             tp = ps_tp.tile([P, 512], F32, name="tp%d" % n, tag="tp")
             st["tp", n] = tp
             for k in range(4):
+                lo = r * 512 + (k // 2) * 256 + k % 2
                 nc.tensor.transpose(
                     out=tp[:, k * P : (k + 1) * P],
-                    in_=adj_w[g][:, r * 512 + (k // 2) * 256 + k % 2 : r * 512 + (k // 2 + 1) * 256 : 2],
+                    in_=adj_w[g][:, lo : lo + 255 : 2],
                     identity=identf[:],
                 )
 
         def a_(n):
-            gt = four.tile([P, N], BF16, name="gt%d" % n, tag="gt", align_bytes=64)
+            gt = gts.tile([P, N], BF16, name="gt%d" % n, tag="gt", align_bytes=64)
             st["gt", n] = gt
             nc.scalar.copy(
                 out=gt[:].bitcast(F32).rearrange("p (c i u) -> p c i u", c=2, u=2),
@@ -140,8 +138,8 @@ def tile_msamodel_pa_kernel(tc, x, adj, w, b, out):
             )
 
         def qa(n):
-            ac = four.tile([P, 256], U32, name="ac%d" % n, tag="ac", align_bytes=64)
-            sc = four.tile([P, 256], U8, name="as%d" % n, tag="as", align_bytes=64)
+            ac = acs.tile([P, 256], U32, name="ac%d" % n, tag="ac", align_bytes=64)
+            sc = acs.tile([P, 256], U8, name="as%d" % n, tag="as", align_bytes=64)
             st["ac", n] = ac
             st["as", n] = sc
             nc.vector.quantize_mx(out=ac[:].bitcast(FP8X4), scales=sc[:], in_=st["gt", n][:])
@@ -166,12 +164,10 @@ def tile_msamodel_pa_kernel(tc, x, adj, w, b, out):
         def b_(n):
             g2 = four.tile([P, D], BF16, name="g2_%d" % n, tag="g2", align_bytes=64)
             st["g2", n] = g2
-            dst = g2[:].rearrange("p (i t) -> p i t", t=4)
-            src = st["p1", n][:].rearrange("p (t i) -> p i t", t=4)
-            if n in B_ON_V:
-                nc.vector.tensor_copy(out=dst, in_=src)
-            else:
-                nc.scalar.copy(out=dst, in_=src)
+            nc.scalar.copy(
+                out=g2[:].rearrange("p (i t) -> p i t", t=4),
+                in_=st["p1", n][:].rearrange("p (t i) -> p i t", t=4),
+            )
 
         def qb(n):
             c2 = four.tile([P, P], U32, name="bc%d" % n, tag="bc", align_bytes=64)
@@ -198,12 +194,15 @@ def tile_msamodel_pa_kernel(tc, x, adj, w, b, out):
             st["z", n] = z
             nc.vector.tensor_tensor(out=z[:], in0=st["p2", n][:], in1=bb[:], op=ALU.add)
 
+        def c2_on_v(n):
+            return n % 3 == 1
+
         def c2(n):
             if ("o", n // 2) not in st:
                 st["o", n // 2] = six.tile([P, 2 * D], F32, name="o%d" % (n // 2), tag="o")
             o = st["o", n // 2][:, (n % 2) * D : (n % 2 + 1) * D]
             rd = r_t[n // 4][:, n % 4 : n % 4 + 1]
-            if n in C2_ON_V:
+            if c2_on_v(n):
                 nc.vector.tensor_scalar(
                     out=o, in0=st["z", n][:], scalar1=rd, scalar2=0.0, op0=ALU.mult, op1=ALU.max
                 )
@@ -236,58 +235,87 @@ def tile_msamodel_pa_kernel(tc, x, adj, w, b, out):
         def pair(m):
             return [2 * m, 2 * m + 1] if 0 <= m < NPAIR else []
 
+        def xrp(g, h):
+            if h == 0:
+                st["xg", g] = two.tile([P, 4 * N], BF16, name="xg%d" % g, tag="xg", align_bytes=64)
+            c, v = divmod(h, 2)
+            dst = st["xg", g][:, h * 1024 : (h + 1) * 1024]
+            src = x_sb[g][:, c * 2048 : (c + 1) * 2048].rearrange("p (j m t) -> p t m j", t=4, j=4)
+            nc.vector.tensor_copy(
+                out=dst.rearrange("p (t m j) -> p t m j", t=2, j=4),
+                in_=src[:, 2 * v : 2 * v + 2, :, :],
+            )
+
+        st["pb"] = ps_p2.tile([P, D], F32, name="pb", tag="p2")
+        nc.tensor.matmul(out=st["pb"][:], lhsT=ones[:], rhs=zb[:], start=True, stop=True)
+        nc.scalar.copy(out=bb[:], in_=st["pb"][:])
         xr(0, 0)
         xr(0, 1)
         xq(0, 0, 1)
         xq(0, 1, 2)
-
-        for s in range(-1, NPAIR + 3):
-            g, q = divmod(s, 4)
-            if s == 2:
-                nc.scalar.copy(out=bb[:], in_=st["pb"][:])
-            for n in pair(s):
-                a_(n)
-            for n in pair(s - 1):
-                dn(n)
-            if s == 1:
-                st["pb"] = ps_p2.tile([P, D], F32, name="pb", tag="p2")
-                nc.tensor.matmul(out=st["pb"][:], lhsT=ones[:], rhs=zb[:], start=True, stop=True)
-            for n in pair(s + 1):
+        for m in range(2):
+            for n in pair(m):
                 t_(n)
-            for n in pair(s - 2):
-                m2(n)
-            for n in pair(s):
-                qa(n)
-            for n in pair(s - 1):
-                b_(n)
-            for n in pair(s):
-                m1(n)
+            for n in pair(m):
+                a_(n)
+        for n in pair(0):
+            qa(n)
+
+        for s in range(NPAIR + 3):
+            g, q = divmod(s, 4)
+            more = g + 1 < G and s < NPAIR
+            for n in pair(s + 2):
+                if s:
+                    a_(n)
             if s == 0:
-                regroup(wg[:], w_sb[:])
-            if s >= 0 and g + 1 < G:
-                if q == 1:
-                    xr(g + 1, 0)
-                if q == 2:
-                    xr(g + 1, 1)
-                if q == 3:
-                    xq(g + 1, 0, 2)
-            if s == 1:
-                nc.vector.quantize_mx(out=wc[:].bitcast(FP8X4), scales=ws[:], in_=wg[:])
-            if 2 <= s <= NPAIR and s % 2 == 0:
-                rb((s - 2) // 2)
-            for n in pair(s - 3):
-                if n in C2_ON_V:
-                    c2(n)
-                    if s - 3 == NPAIR - 1:
-                        store(s - 3, n % 2, n % 2 + 1)
-            for n in pair(s - 1):
-                qb(n)
+                for n in pair(1):
+                    qa(n)
+            for n in pair(s)[0:1]:
+                m1(n)
+            for n in pair(s - 1)[0:1]:
+                dn(n)
+            for n in pair(s)[1:2]:
+                m1(n)
+            for n in pair(s - 1)[1:2]:
+                dn(n)
             for n in pair(s - 2):
                 c1(n)
+            if s == 0:
+                for n in pair(2):
+                    t_(n)
+                for n in pair(2):
+                    a_(n)
+            for n in pair(s + 3):
+                t_(n)
+            for n in pair(s - 1):
+                qb(n)
             for n in pair(s - 3):
-                if n not in C2_ON_V:
+                if not c2_on_v(n):
                     c2(n)
-                    if s - 3 == NPAIR - 1:
-                        store(s - 3, n % 2, n % 2 + 1)
-            if 0 <= s - 3 < NPAIR - 1:
+            if s == 0:
+                regroup(wg[:], w_sb[:])
+            for n in pair(s - 1):
+                m2(n)
+            if more and q == 1:
+                xrp(g + 1, 0)
+            if more and q == 2:
+                xrp(g + 1, 1)
+                xrp(g + 1, 2)
+            if more and q == 3:
+                xq(g + 1, 0, 1)
+                xrp(g + 1, 3)
+            for n in pair(s):
+                b_(n)
+            for n in pair(s - 3):
+                if c2_on_v(n):
+                    c2(n)
+            if 0 <= s - 3 < NPAIR:
                 store(s - 3, 0, 2)
+            if more and q == 3:
+                xq(g + 1, 1, 2)
+            for n in pair(s + 2):
+                qa(n)
+            if s == 0:
+                nc.vector.quantize_mx(out=wc[:].bitcast(FP8X4), scales=ws[:], in_=wg[:])
+            if s >= 2 and s % 2 == 0 and s <= NPAIR:
+                rb(s // 2 - 1)

@@ -65,12 +65,11 @@ def tile_msamodel_pa_kernel(tc, x, adj, w, b, out):
             )
 
         nc.vector.memset(zb[:], 0.0)
-        nc.scalar.dma_start(out=zb[0:1, :], in_=b.rearrange("(o n) -> o n", o=1))
-
         load_x(0, 0, 1)
-        load_adj(0, 0, 1)
         load_x(0, 1, 2)
+        load_adj(0, 0, 1)
         load_adj(0, 1, 2)
+        nc.sync.dma_start(out=zb[0:1, :], in_=b.rearrange("(o n) -> o n", o=1))
         load_adj(0, 2, 4)
         load_adj(0, 4, 6)
         nc.sync.dma_start(out=w_sb[:], in_=w.rearrange("(p t) e -> p (t e)", t=4))
@@ -246,9 +245,6 @@ def tile_msamodel_pa_kernel(tc, x, adj, w, b, out):
                 in_=src[:, 2 * v : 2 * v + 2, :, :],
             )
 
-        st["pb"] = ps_p2.tile([P, D], F32, name="pb", tag="p2")
-        nc.tensor.matmul(out=st["pb"][:], lhsT=ones[:], rhs=zb[:], start=True, stop=True)
-        nc.scalar.copy(out=bb[:], in_=st["pb"][:])
         xr(0, 0)
         xr(0, 1)
         xq(0, 0, 1)
@@ -272,29 +268,31 @@ def tile_msamodel_pa_kernel(tc, x, adj, w, b, out):
                     qa(n)
             for n in pair(s)[0:1]:
                 m1(n)
-            for n in pair(s - 1)[0:1]:
+            for n in pair(s - 1):
                 dn(n)
             for n in pair(s)[1:2]:
                 m1(n)
-            for n in pair(s - 1)[1:2]:
-                dn(n)
             for n in pair(s - 2):
                 c1(n)
+            for n in pair(s - 1):
+                qb(n)
+            for n in pair(s - 1)[0:1]:
+                m2(n)
             if s == 0:
+                st["pb"] = ps_p2.tile([P, D], F32, name="pb", tag="p2")
+                nc.tensor.matmul(out=st["pb"][:], lhsT=ones[:], rhs=zb[:], start=True, stop=True)
                 for n in pair(2):
                     t_(n)
                 for n in pair(2):
                     a_(n)
             for n in pair(s + 3):
                 t_(n)
-            for n in pair(s - 1):
-                qb(n)
             for n in pair(s - 3):
                 if not c2_on_v(n):
                     c2(n)
             if s == 0:
                 regroup(wg[:], w_sb[:])
-            for n in pair(s - 1):
+            for n in pair(s - 1)[1:2]:
                 m2(n)
             if more and q == 1:
                 xrp(g + 1, 0)
@@ -306,6 +304,8 @@ def tile_msamodel_pa_kernel(tc, x, adj, w, b, out):
                 xrp(g + 1, 3)
             for n in pair(s):
                 b_(n)
+            if s == 0:
+                nc.scalar.copy(out=bb[:], in_=st["pb"][:])
             for n in pair(s - 3):
                 if c2_on_v(n):
                     c2(n)

@@ -27,10 +27,11 @@ def tile_msamodel_pa_kernel(tc, x, adj, w, b, out):
     with ExitStack() as ctx:
         const = ctx.enter_context(tc.tile_pool(name="const", bufs=1))
         two = ctx.enter_context(tc.tile_pool(name="two", bufs=2))
-        gts = ctx.enter_context(tc.tile_pool(name="gts", bufs=10))
-        acs = ctx.enter_context(tc.tile_pool(name="acs", bufs=8))
+        three = ctx.enter_context(tc.tile_pool(name="three", bufs=3))
         four = ctx.enter_context(tc.tile_pool(name="four", bufs=4))
-        six = ctx.enter_context(tc.tile_pool(name="six", bufs=5))
+        five = ctx.enter_context(tc.tile_pool(name="five", bufs=5))
+        gts = ctx.enter_context(tc.tile_pool(name="gts", bufs=6))
+        zs = ctx.enter_context(tc.tile_pool(name="zs", bufs=8))
         ps_tp = ctx.enter_context(tc.psum_pool(name="ps_tp", bufs=2))
         ps_p1 = ctx.enter_context(tc.psum_pool(name="ps_p1", bufs=3))
         ps_p2 = ctx.enter_context(tc.psum_pool(name="ps_p2", bufs=2))
@@ -52,8 +53,11 @@ def tile_msamodel_pa_kernel(tc, x, adj, w, b, out):
         ones = const.tile([P, P], BF16, name="ones")
         identf = const.tile([P, P], F32, name="identf")
         bb = const.tile([P, D], F32, name="bb")
-        e_t = [const.tile([P, 4], F32, name="e_t%d" % k) for k in range(NU // 4)]
-        r_t = [const.tile([P, 4], F32, name="r_t%d" % k) for k in range(NU // 4)]
+        sel = const.tile([P, 7 * 32], F32, name="sel")
+        dd = [const.tile([P, 32], F32, name="dd%d" % g) for g in range(G)]
+        e_t = [const.tile([P, R], F32, name="e_t%d" % g) for g in range(G)]
+        r_t = [const.tile([P, R], F32, name="r_t%d" % g) for g in range(G)]
+        pd = ps_pd.tile([P, 80], F32, name="pd")
 
         def load_adj(g, r0, r1):
             nc.sync.dma_start(out=adj_sb[g][:, r0 * N : r1 * N], in_=adj_v[g, :, r0 * N : r1 * N])
@@ -86,6 +90,10 @@ def tile_msamodel_pa_kernel(tc, x, adj, w, b, out):
 
         nc.vector.memset(ones[:], 1.0)
         make_identity(nc, identf[:])
+        nc.vector.memset(sel[:], 0.0)
+        nc.vector.tensor_reduce(
+            out=sel[:, 96:128], in_=identf[:].rearrange("p (i t) -> p i t", t=4), axis=AX.X, op=ALU.add
+        )
 
         st = {}
 
@@ -95,16 +103,24 @@ def tile_msamodel_pa_kernel(tc, x, adj, w, b, out):
                 in_=src.rearrange("p (t c i) -> p c t i", t=4, i=4),
             )
 
-        def regroup_x(dst, src):
-            nc.vector.tensor_copy(
-                out=dst.rearrange("p (t m j) -> p t m j", t=4, j=4),
-                in_=src.rearrange("p (j m t) -> p t m j", t=4, j=4),
-            )
-
-        def xr(g, c):
-            if c == 0:
+        def xr(g, h, eng):
+            if ("xg", g) not in st:
                 st["xg", g] = two.tile([P, 4 * N], BF16, name="xg%d" % g, tag="xg", align_bytes=64)
-            regroup_x(st["xg", g][:, c * 2048 : (c + 1) * 2048], x_sb[g][:, c * 2048 : (c + 1) * 2048])
+            c, v = divmod(h, 2)
+            dst = st["xg", g][:, h * 1024 : (h + 1) * 1024].rearrange("p (t m j) -> p t m j", t=2, j=4)
+            src = x_sb[g][:, c * 2048 : (c + 1) * 2048].rearrange("p (j m t) -> p t m j", t=4, j=4)
+            if eng == "s":
+                nc.scalar.copy(out=dst, in_=src[:, 2 * v : 2 * v + 2, :, :])
+            else:
+                nc.vector.tensor_copy(out=dst, in_=src[:, 2 * v : 2 * v + 2, :, :])
+
+        def xr2(g, c):
+            if ("xg", g) not in st:
+                st["xg", g] = two.tile([P, 4 * N], BF16, name="xg%d" % g, tag="xg", align_bytes=64)
+            nc.vector.tensor_copy(
+                out=st["xg", g][:, c * 2048 : (c + 1) * 2048].rearrange("p (t m j) -> p t m j", t=4, j=4),
+                in_=x_sb[g][:, c * 2048 : (c + 1) * 2048].rearrange("p (j m t) -> p t m j", t=4, j=4),
+            )
 
         def xq(g, c0, c1):
             if c0 == 0:
@@ -129,59 +145,62 @@ def tile_msamodel_pa_kernel(tc, x, adj, w, b, out):
                 )
 
         def a_(n):
-            gt = gts.tile([P, N], BF16, name="gt%d" % n, tag="gt", align_bytes=64)
-            st["gt", n] = gt
+            m, h = divmod(n, 2)
+            if h == 0:
+                st["gt", m] = gts.tile([P, 2 * N], BF16, name="gt%d" % m, tag="gt", align_bytes=64)
             nc.scalar.copy(
-                out=gt[:].bitcast(F32).rearrange("p (c i u) -> p c i u", c=2, u=2),
+                out=st["gt", m][:, h * N : (h + 1) * N].bitcast(F32).rearrange("p (c i u) -> p c i u", c=2, u=2),
                 in_=st["tp", n][:].rearrange("p (c u i) -> p c i u", c=2, u=2),
             )
 
-        def qa(n):
-            ac = acs.tile([P, 256], U32, name="ac%d" % n, tag="ac", align_bytes=64)
-            sc = acs.tile([P, 256], U8, name="as%d" % n, tag="as", align_bytes=64)
-            st["ac", n] = ac
-            st["as", n] = sc
-            nc.vector.quantize_mx(out=ac[:].bitcast(FP8X4), scales=sc[:], in_=st["gt", n][:])
+        def qa(m):
+            st["ac", m] = four.tile([P, 512], U32, name="ac%d" % m, tag="ac", align_bytes=64)
+            st["as", m] = four.tile([P, 512], U8, name="as%d" % m, tag="as", align_bytes=64)
+            nc.vector.quantize_mx(out=st["ac", m][:].bitcast(FP8X4), scales=st["as", m][:], in_=st["gt", m][:])
 
         def m1(n):
             g = n // R
+            m, h = divmod(n, 2)
             p1 = ps_p1.tile([P, 512], F32, name="p1_%d" % n, tag="p1")
             st["p1", n] = p1
             for t in range(4):
                 for c in range(2):
                     lo = c * D + t * P
+                    ro = (2 * h + c) * P
                     nc.tensor.matmul_mx(
                         out=p1[:, t * P : (t + 1) * P],
                         lhsT=st["xc", g][:, lo : lo + P].bitcast(FP8X4),
                         lhsT_scale=st["xs", g][:, lo : lo + P],
-                        rhs=st["ac", n][:, c * P : (c + 1) * P].bitcast(FP8X4),
-                        rhs_scale=st["as", n][:, c * P : (c + 1) * P],
+                        rhs=st["ac", m][:, ro : ro + P].bitcast(FP8X4),
+                        rhs_scale=st["as", m][:, ro : ro + P],
                         start=(c == 0),
                         stop=(c == 1),
                     )
 
-        def b_(n):
-            g2 = four.tile([P, D], BF16, name="g2_%d" % n, tag="g2", align_bytes=64)
-            st["g2", n] = g2
-            nc.scalar.copy(
-                out=g2[:].rearrange("p (i t) -> p i t", t=4),
-                in_=st["p1", n][:].rearrange("p (t i) -> p i t", t=4),
-            )
+        def b_(n, on_v=False):
+            m, h = divmod(n, 2)
+            if h == 0:
+                st["g2", m] = three.tile([P, 2 * D], BF16, name="g2_%d" % m, tag="g2", align_bytes=64)
+            dst = st["g2", m][:, h * D : (h + 1) * D].rearrange("p (i t) -> p i t", t=4)
+            src = st["p1", n][:].rearrange("p (t i) -> p i t", t=4)
+            if on_v:
+                nc.vector.tensor_copy(out=dst, in_=src)
+            else:
+                nc.scalar.copy(out=dst, in_=src)
 
-        def qb(n):
-            c2 = four.tile([P, P], U32, name="bc%d" % n, tag="bc", align_bytes=64)
-            s2 = four.tile([P, P], U8, name="bs%d" % n, tag="bs", align_bytes=64)
-            st["bc", n] = c2
-            st["bs", n] = s2
-            nc.vector.quantize_mx(out=c2[:].bitcast(FP8X4), scales=s2[:], in_=st["g2", n][:])
+        def qb(m):
+            st["bc", m] = three.tile([P, 2 * P], U32, name="bc%d" % m, tag="bc", align_bytes=64)
+            st["bs", m] = three.tile([P, 2 * P], U8, name="bs%d" % m, tag="bs", align_bytes=64)
+            nc.vector.quantize_mx(out=st["bc", m][:].bitcast(FP8X4), scales=st["bs", m][:], in_=st["g2", m][:])
 
         def m2(n):
+            m, h = divmod(n, 2)
             p2 = ps_p2.tile([P, D], F32, name="p2_%d" % n, tag="p2")
             st["p2", n] = p2
             nc.tensor.matmul_mx(
                 out=p2[:],
-                lhsT=st["bc", n][:].bitcast(FP8X4),
-                lhsT_scale=st["bs", n][:],
+                lhsT=st["bc", m][:, h * P : (h + 1) * P].bitcast(FP8X4),
+                lhsT_scale=st["bs", m][:, h * P : (h + 1) * P],
                 rhs=wc[:].bitcast(FP8X4),
                 rhs_scale=ws[:],
                 start=True,
@@ -189,7 +208,7 @@ def tile_msamodel_pa_kernel(tc, x, adj, w, b, out):
             )
 
         def c1(n):
-            z = four.tile([P, D], F32, name="z%d" % n, tag="z")
+            z = zs.tile([P, D], F32, name="z%d" % n, tag="z")
             st["z", n] = z
             nc.vector.tensor_tensor(out=z[:], in0=st["p2", n][:], in1=bb[:], op=ALU.add)
 
@@ -197,10 +216,11 @@ def tile_msamodel_pa_kernel(tc, x, adj, w, b, out):
             return n % 3 == 1
 
         def c2(n):
-            if ("o", n // 2) not in st:
-                st["o", n // 2] = six.tile([P, 2 * D], F32, name="o%d" % (n // 2), tag="o")
-            o = st["o", n // 2][:, (n % 2) * D : (n % 2 + 1) * D]
-            rd = r_t[n // 4][:, n % 4 : n % 4 + 1]
+            m, h = divmod(n, 2)
+            if ("o", m) not in st:
+                st["o", m] = five.tile([P, 2 * D], F32, name="o%d" % m, tag="o")
+            o = st["o", m][:, h * D : (h + 1) * D]
+            rd = r_t[n // R][:, n % R : n % R + 1]
             if c2_on_v(n):
                 nc.vector.tensor_scalar(
                     out=o, in0=st["z", n][:], scalar1=rd, scalar2=0.0, op0=ALU.mult, op1=ALU.max
@@ -215,38 +235,45 @@ def tile_msamodel_pa_kernel(tc, x, adj, w, b, out):
             )
 
         def dn(n):
-            if n % 4 == 0:
-                st["pd", n // 4] = ps_pd.tile([P, 4], F32, name="pd%d" % (n // 4), tag="pd")
-            cols = st["gt", n][:].rearrange("p (c i t) -> p c t i", c=2, t=4)
-            for k in range(8):
+            g, q = divmod(n, R)
+            m, h = divmod(n, 2)
+            base = 40 * (g % 2)
+            for v in range(4):
+                for c in range(2):
+                    lo = h * N + c * 512 + v * P
+                    nc.tensor.matmul(
+                        out=pd[:, base + v * R + q : base + v * R + q + 1],
+                        lhsT=st["gt", m][:, lo : lo + P],
+                        rhs=ones[:, 0:1],
+                        start=(c == 0),
+                        stop=(c == 1),
+                    )
+
+        def dcopy(g):
+            base = 40 * (g % 2)
+            nc.vector.tensor_copy(out=dd[g][:], in_=pd[:, base : base + 32])
+
+        def dsel(g):
+            base = 40 * (g % 2)
+            for v in range(4):
                 nc.tensor.matmul(
-                    out=st["pd", n // 4][:, n % 4 : n % 4 + 1],
-                    lhsT=cols[:, k // 4, k % 4, :],
-                    rhs=ones[:, 0:1],
-                    start=(k == 0),
-                    stop=(k == 7),
+                    out=pd[:, base + 32 : base + 40],
+                    lhsT=sel[:, 96 - 32 * v : 224 - 32 * v],
+                    rhs=dd[g][:, v * R : (v + 1) * R],
+                    start=(v == 0),
+                    stop=(v == 3),
                 )
 
-        def rb(k):
-            nc.vector.tensor_scalar_add(out=e_t[k][:], in0=st["pd", k][:], scalar1=1.0)
-            nc.vector.reciprocal(out=r_t[k][:], in_=e_t[k][:])
+        def rb(g):
+            base = 40 * (g % 2)
+            nc.vector.tensor_scalar_add(out=e_t[g][:], in0=pd[:, base + 32 : base + 40], scalar1=1.0)
+            nc.vector.reciprocal(out=r_t[g][:], in_=e_t[g][:])
 
         def pair(m):
             return [2 * m, 2 * m + 1] if 0 <= m < NPAIR else []
 
-        def xrp(g, h):
-            if h == 0:
-                st["xg", g] = two.tile([P, 4 * N], BF16, name="xg%d" % g, tag="xg", align_bytes=64)
-            c, v = divmod(h, 2)
-            dst = st["xg", g][:, h * 1024 : (h + 1) * 1024]
-            src = x_sb[g][:, c * 2048 : (c + 1) * 2048].rearrange("p (j m t) -> p t m j", t=4, j=4)
-            nc.vector.tensor_copy(
-                out=dst.rearrange("p (t m j) -> p t m j", t=2, j=4),
-                in_=src[:, 2 * v : 2 * v + 2, :, :],
-            )
-
-        xr(0, 0)
-        xr(0, 1)
+        xr2(0, 0)
+        xr2(0, 1)
         xq(0, 0, 1)
         xq(0, 1, 2)
         for m in range(2):
@@ -254,28 +281,35 @@ def tile_msamodel_pa_kernel(tc, x, adj, w, b, out):
                 t_(n)
             for n in pair(m):
                 a_(n)
-        for n in pair(0):
-            qa(n)
+        qa(0)
 
-        for s in range(NPAIR + 3):
+        for s in range(NPAIR + 2):
             g, q = divmod(s, 4)
-            more = g + 1 < G and s < NPAIR
-            for n in pair(s + 2):
-                if s:
+            more = g + 1 < G
+            if s > 0:
+                for n in pair(s + 2):
                     a_(n)
             if s == 0:
-                for n in pair(1):
-                    qa(n)
+                qa(1)
+            if q == 3 and s < NPAIR:
+                dcopy(g)
+            if more and (q == 3 or g > 0):
+                xr(g + 1, q, "v")
             for n in pair(s)[0:1]:
                 m1(n)
-            for n in pair(s - 1):
+            if s == 0:
+                for n in pair(0):
+                    dn(n)
+            for n in pair(s + 1):
                 dn(n)
             for n in pair(s)[1:2]:
                 m1(n)
+            if q == 3 and s < NPAIR:
+                dsel(g)
             for n in pair(s - 2):
                 c1(n)
-            for n in pair(s - 1):
-                qb(n)
+            if 0 <= s - 1 < NPAIR:
+                qb(s - 1)
             for n in pair(s - 1)[0:1]:
                 m2(n)
             if s == 0:
@@ -287,35 +321,35 @@ def tile_msamodel_pa_kernel(tc, x, adj, w, b, out):
                     a_(n)
             for n in pair(s + 3):
                 t_(n)
-            for n in pair(s - 3):
-                if not c2_on_v(n):
-                    c2(n)
+            done = [s - 4] if s < NPAIR else [[12, 13, 14], [15]][s - NPAIR]
+            for m in done:
+                for n in pair(m):
+                    if not c2_on_v(n):
+                        c2(n)
             if s == 0:
                 regroup(wg[:], w_sb[:])
             for n in pair(s - 1)[1:2]:
                 m2(n)
-            if more and q == 1:
-                xrp(g + 1, 0)
-            if more and q == 2:
-                xrp(g + 1, 1)
-                xrp(g + 1, 2)
+            if more and g == 0 and q == 1:
+                xr(1, 0, "v")
+            if more and g == 0 and q == 2:
+                xr(1, 1, "v")
+                xr(1, 2, "v")
             if more and q == 3:
-                xq(g + 1, 0, 1)
-                xrp(g + 1, 3)
+                xq(g + 1, 0, 2)
             for n in pair(s):
                 b_(n)
             if s == 0:
                 nc.scalar.copy(out=bb[:], in_=st["pb"][:])
-            for n in pair(s - 3):
-                if c2_on_v(n):
-                    c2(n)
-            if 0 <= s - 3 < NPAIR:
-                store(s - 3, 0, 2)
-            if more and q == 3:
-                xq(g + 1, 1, 2)
-            for n in pair(s + 2):
-                qa(n)
+            for m in done:
+                for n in pair(m):
+                    if c2_on_v(n):
+                        c2(n)
+                if m >= 0:
+                    store(m, 0, 2)
+            if s + 2 < NPAIR:
+                qa(s + 2)
+            if q == 3 and s < NPAIR:
+                rb(g)
             if s == 0:
                 nc.vector.quantize_mx(out=wc[:].bitcast(FP8X4), scales=ws[:], in_=wg[:])
-            if s >= 2 and s % 2 == 0 and s <= NPAIR:
-                rb(s // 2 - 1)

@@ -107,19 +107,20 @@ def tile_msamodel_pa_kernel(tc, x, adj, w, b, out):
             if ("xg", g) not in st:
                 st["xg", g] = two.tile([P, 4 * N], BF16, name="xg%d" % g, tag="xg", align_bytes=64)
             c, v = divmod(h, 2)
-            dst = st["xg", g][:, h * 1024 : (h + 1) * 1024].rearrange("p (t m j) -> p t m j", t=2, j=4)
-            src = x_sb[g][:, c * 2048 : (c + 1) * 2048].rearrange("p (j m t) -> p t m j", t=4, j=4)
+            cols = slice(c * 2048, (c + 1) * 2048)
+            dst = st["xg", g][:, cols].rearrange("p (t m j) -> p m j t", t=4, j=4)[:, v * 64 : (v + 1) * 64, :, :]
+            src = x_sb[g][:, cols].rearrange("p (j m t) -> p m j t", t=4, j=4)[:, v * 64 : (v + 1) * 64, :, :]
             if eng == "s":
-                nc.scalar.copy(out=dst, in_=src[:, 2 * v : 2 * v + 2, :, :])
+                nc.scalar.copy(out=dst, in_=src)
             else:
-                nc.vector.tensor_copy(out=dst, in_=src[:, 2 * v : 2 * v + 2, :, :])
+                nc.vector.tensor_copy(out=dst, in_=src)
 
         def xr2(g, c):
             if ("xg", g) not in st:
                 st["xg", g] = two.tile([P, 4 * N], BF16, name="xg%d" % g, tag="xg", align_bytes=64)
             nc.vector.tensor_copy(
-                out=st["xg", g][:, c * 2048 : (c + 1) * 2048].rearrange("p (t m j) -> p t m j", t=4, j=4),
-                in_=x_sb[g][:, c * 2048 : (c + 1) * 2048].rearrange("p (j m t) -> p t m j", t=4, j=4),
+                out=st["xg", g][:, c * 2048 : (c + 1) * 2048].rearrange("p (t m j) -> p m j t", t=4, j=4),
+                in_=x_sb[g][:, c * 2048 : (c + 1) * 2048].rearrange("p (j m t) -> p m j t", t=4, j=4),
             )
 
         def xq(g, c0, c1):

@@ -10,7 +10,6 @@ U8 = mybir.dt.uint8
 FP8X4 = mybir.dt.float8_e4m3fn_x4
 ALU = mybir.AluOpType
 ACT = mybir.ActivationFunctionType
-AX = mybir.AxisListType
 
 G = 4
 N = 1024
@@ -31,7 +30,7 @@ def tile_msamodel_pa_kernel(tc, x, adj, w, b, out):
         four = ctx.enter_context(tc.tile_pool(name="four", bufs=4))
         five = ctx.enter_context(tc.tile_pool(name="five", bufs=5))
         gts = ctx.enter_context(tc.tile_pool(name="gts", bufs=6))
-        zs = ctx.enter_context(tc.tile_pool(name="zs", bufs=8))
+        zs = ctx.enter_context(tc.tile_pool(name="zs", bufs=5))
         ps_tp = ctx.enter_context(tc.psum_pool(name="ps_tp", bufs=2))
         ps_p1 = ctx.enter_context(tc.psum_pool(name="ps_p1", bufs=3))
         ps_p2 = ctx.enter_context(tc.psum_pool(name="ps_p2", bufs=2))
@@ -53,11 +52,9 @@ def tile_msamodel_pa_kernel(tc, x, adj, w, b, out):
         ones = const.tile([P, P], BF16, name="ones")
         identf = const.tile([P, P], F32, name="identf")
         bb = const.tile([P, D], F32, name="bb")
-        sel = const.tile([P, 7 * 32], F32, name="sel")
-        dd = [const.tile([P, 32], F32, name="dd%d" % g) for g in range(G)]
-        e_t = [const.tile([P, R], F32, name="e_t%d" % g) for g in range(G)]
-        r_t = [const.tile([P, R], F32, name="r_t%d" % g) for g in range(G)]
-        pd = ps_pd.tile([P, 80], F32, name="pd")
+        e_t = [const.tile([P, 4], F32, name="e_t%d" % k) for k in range(NU // 4)]
+        r_t = [const.tile([P, 4], F32, name="r_t%d" % k) for k in range(NU // 4)]
+        pd = ps_pd.tile([P, NU], F32, name="pd")
 
         def load_adj(g, r0, r1):
             nc.sync.dma_start(out=adj_sb[g][:, r0 * N : r1 * N], in_=adj_v[g, :, r0 * N : r1 * N])
@@ -90,10 +87,6 @@ def tile_msamodel_pa_kernel(tc, x, adj, w, b, out):
 
         nc.vector.memset(ones[:], 1.0)
         make_identity(nc, identf[:])
-        nc.vector.memset(sel[:], 0.0)
-        nc.vector.tensor_reduce(
-            out=sel[:, 96:128], in_=identf[:].rearrange("p (i t) -> p i t", t=4), axis=AX.X, op=ALU.add
-        )
 
         st = {}
 
@@ -154,10 +147,15 @@ def tile_msamodel_pa_kernel(tc, x, adj, w, b, out):
                 in_=st["tp", n][:].rearrange("p (c u i) -> p c i u", c=2, u=2),
             )
 
-        def qa(m):
-            st["ac", m] = four.tile([P, 512], U32, name="ac%d" % m, tag="ac", align_bytes=64)
-            st["as", m] = four.tile([P, 512], U8, name="as%d" % m, tag="as", align_bytes=64)
-            nc.vector.quantize_mx(out=st["ac", m][:].bitcast(FP8X4), scales=st["as", m][:], in_=st["gt", m][:])
+        def qa(m, h0=0, h1=2):
+            if h0 == 0:
+                st["ac", m] = four.tile([P, 512], U32, name="ac%d" % m, tag="ac", align_bytes=64)
+                st["as", m] = four.tile([P, 512], U8, name="as%d" % m, tag="as", align_bytes=64)
+            nc.vector.quantize_mx(
+                out=st["ac", m][:, h0 * 256 : h1 * 256].bitcast(FP8X4),
+                scales=st["as", m][:, h0 * 256 : h1 * 256],
+                in_=st["gt", m][:, h0 * N : h1 * N],
+            )
 
         def m1(n):
             g = n // R
@@ -189,14 +187,22 @@ def tile_msamodel_pa_kernel(tc, x, adj, w, b, out):
             else:
                 nc.scalar.copy(out=dst, in_=src)
 
-        def qb(m):
-            st["bc", m] = three.tile([P, 2 * P], U32, name="bc%d" % m, tag="bc", align_bytes=64)
-            st["bs", m] = three.tile([P, 2 * P], U8, name="bs%d" % m, tag="bs", align_bytes=64)
-            nc.vector.quantize_mx(out=st["bc", m][:].bitcast(FP8X4), scales=st["bs", m][:], in_=st["g2", m][:])
+        def qb(m, h0=0, h1=2):
+            if h0 == 0:
+                st["bc", m] = three.tile([P, 2 * P], U32, name="bc%d" % m, tag="bc", align_bytes=64)
+                st["bs", m] = three.tile([P, 2 * P], U8, name="bs%d" % m, tag="bs", align_bytes=64)
+            nc.vector.quantize_mx(
+                out=st["bc", m][:, h0 * P : h1 * P].bitcast(FP8X4),
+                scales=st["bs", m][:, h0 * P : h1 * P],
+                in_=st["g2", m][:, h0 * D : h1 * D],
+            )
 
         def m2(n):
             m, h = divmod(n, 2)
-            p2 = ps_p2.tile([P, D], F32, name="p2_%d" % n, tag="p2")
+            if m in (NPAIR - 3, NPAIR - 1):
+                p2 = ps_tp.tile([P, D], F32, name="p2_%d" % n, tag="tp")
+            else:
+                p2 = ps_p2.tile([P, D], F32, name="p2_%d" % n, tag="p2")
             st["p2", n] = p2
             nc.tensor.matmul_mx(
                 out=p2[:],
@@ -214,14 +220,14 @@ def tile_msamodel_pa_kernel(tc, x, adj, w, b, out):
             nc.vector.tensor_tensor(out=z[:], in0=st["p2", n][:], in1=bb[:], op=ALU.add)
 
         def c2_on_v(n):
-            return n % 3 == 1
+            return n % 6 == 1
 
         def c2(n):
             m, h = divmod(n, 2)
             if ("o", m) not in st:
                 st["o", m] = five.tile([P, 2 * D], F32, name="o%d" % m, tag="o")
             o = st["o", m][:, h * D : (h + 1) * D]
-            rd = r_t[n // R][:, n % R : n % R + 1]
+            rd = r_t[n // 4][:, n % 4 : n % 4 + 1]
             if c2_on_v(n):
                 nc.vector.tensor_scalar(
                     out=o, in0=st["z", n][:], scalar1=rd, scalar2=0.0, op0=ALU.mult, op1=ALU.max
@@ -236,39 +242,20 @@ def tile_msamodel_pa_kernel(tc, x, adj, w, b, out):
             )
 
         def dn(n):
-            g, q = divmod(n, R)
             m, h = divmod(n, 2)
-            base = 40 * (g % 2)
-            for v in range(4):
-                for c in range(2):
-                    lo = h * N + c * 512 + v * P
-                    nc.tensor.matmul(
-                        out=pd[:, base + v * R + q : base + v * R + q + 1],
-                        lhsT=st["gt", m][:, lo : lo + P],
-                        rhs=ones[:, 0:1],
-                        start=(c == 0),
-                        stop=(c == 1),
-                    )
-
-        def dcopy(g):
-            base = 40 * (g % 2)
-            nc.vector.tensor_copy(out=dd[g][:], in_=pd[:, base : base + 32])
-
-        def dsel(g):
-            base = 40 * (g % 2)
-            for v in range(4):
+            cols = st["gt", m][:, h * N : (h + 1) * N].rearrange("p (c i t) -> p c t i", c=2, t=4)
+            for k in range(8):
                 nc.tensor.matmul(
-                    out=pd[:, base + 32 : base + 40],
-                    lhsT=sel[:, 96 - 32 * v : 224 - 32 * v],
-                    rhs=dd[g][:, v * R : (v + 1) * R],
-                    start=(v == 0),
-                    stop=(v == 3),
+                    out=pd[:, n : n + 1],
+                    lhsT=cols[:, k // 4, k % 4, :],
+                    rhs=ones[:, 0:1],
+                    start=(k == 0),
+                    stop=(k == 7),
                 )
 
-        def rb(g):
-            base = 40 * (g % 2)
-            nc.vector.tensor_scalar_add(out=e_t[g][:], in0=pd[:, base + 32 : base + 40], scalar1=1.0)
-            nc.vector.reciprocal(out=r_t[g][:], in_=e_t[g][:])
+        def rb(k):
+            nc.vector.tensor_scalar_add(out=e_t[k][:], in0=pd[:, 4 * k : 4 * k + 4], scalar1=1.0)
+            nc.vector.reciprocal(out=r_t[k][:], in_=e_t[k][:])
 
         def pair(m):
             return [2 * m, 2 * m + 1] if 0 <= m < NPAIR else []
@@ -280,37 +267,35 @@ def tile_msamodel_pa_kernel(tc, x, adj, w, b, out):
         for m in range(2):
             for n in pair(m):
                 t_(n)
-            for n in pair(m):
                 a_(n)
-        qa(0)
+        qa(0, 0, 1)
+        qa(0, 1, 2)
 
         for s in range(NPAIR + 2):
             g, q = divmod(s, 4)
             more = g + 1 < G
-            if s > 0:
-                for n in pair(s + 2):
-                    a_(n)
-            if s == 0:
-                qa(1)
-            if q == 3 and s < NPAIR:
-                dcopy(g)
-            if more and (q == 3 or g > 0):
-                xr(g + 1, q, "v")
+            last = s == NPAIR - 1
+            done = [s - 2]
             for n in pair(s)[0:1]:
                 m1(n)
             if s == 0:
                 for n in pair(0):
                     dn(n)
+            if s > 0:
+                for n in pair(s + 2):
+                    a_(n)
+            else:
+                qa(1)
             for n in pair(s + 1):
                 dn(n)
             for n in pair(s)[1:2]:
                 m1(n)
-            if q == 3 and s < NPAIR:
-                dsel(g)
-            for n in pair(s - 2):
-                c1(n)
             if 0 <= s - 1 < NPAIR:
                 qb(s - 1)
+            for n in pair(s - 2):
+                c1(n)
+            for n in pair(s)[0:1]:
+                b_(n)
             for n in pair(s - 1)[0:1]:
                 m2(n)
             if s == 0:
@@ -322,35 +307,37 @@ def tile_msamodel_pa_kernel(tc, x, adj, w, b, out):
                     a_(n)
             for n in pair(s + 3):
                 t_(n)
-            done = [s - 4] if s < NPAIR else [[12, 13, 14], [15]][s - NPAIR]
-            for m in done:
-                for n in pair(m):
-                    if not c2_on_v(n):
-                        c2(n)
+            for n in pair(s - 2)[0:1]:
+                if not c2_on_v(n):
+                    c2(n)
             if s == 0:
                 regroup(wg[:], w_sb[:])
             for n in pair(s - 1)[1:2]:
                 m2(n)
+            if more and (q == 3 or g > 0):
+                xr(g + 1, q, "v")
             if more and g == 0 and q == 1:
                 xr(1, 0, "v")
             if more and g == 0 and q == 2:
                 xr(1, 1, "v")
                 xr(1, 2, "v")
-            if more and q == 3:
-                xq(g + 1, 0, 2)
-            for n in pair(s):
-                b_(n)
+            for n in pair(s)[1:2]:
+                b_(n, last)
             if s == 0:
                 nc.scalar.copy(out=bb[:], in_=st["pb"][:])
-            for m in done:
-                for n in pair(m):
-                    if c2_on_v(n):
-                        c2(n)
-                if m >= 0:
-                    store(m, 0, 2)
+            for n in pair(s - 2)[1:2]:
+                if not c2_on_v(n):
+                    c2(n)
+            for n in pair(s - 2):
+                if c2_on_v(n):
+                    c2(n)
+            if 0 <= s - 2:
+                store(s - 2, 0, 2)
             if s + 2 < NPAIR:
                 qa(s + 2)
-            if q == 3 and s < NPAIR:
-                rb(g)
+            if more and q == 3:
+                xq(g + 1, 0, 2)
+            if s % 2 == 0 and s < NPAIR:
+                rb(s // 2)
             if s == 0:
                 nc.vector.quantize_mx(out=wc[:].bitcast(FP8X4), scales=ws[:], in_=wg[:])

@@ -131,12 +131,21 @@ def tile_msamodel_pa_kernel(tc, x, adj, w, b, out):
             tp = ps_tp.tile([P, 512], F32, name="tp%d" % n, tag="tp")
             st["tp", n] = tp
             for k in range(4):
-                lo = r * 512 + (k // 2) * 256 + k % 2
-                nc.tensor.transpose(
-                    out=tp[:, k * P : (k + 1) * P],
-                    in_=adj_w[g][:, lo : lo + 255 : 2],
-                    identity=identf[:],
-                )
+                if ("di", n // 2) in st:
+                    lo = (n % 2) * 512 + k * P
+                    words = st["di", n // 2][:, lo : lo + P]
+                else:
+                    lo = r * 512 + (k // 2) * 256 + k % 2
+                    words = adj_w[g][:, lo : lo + 255 : 2]
+                nc.tensor.transpose(out=tp[:, k * P : (k + 1) * P], in_=words, identity=identf[:])
+
+        def di(m):
+            g, k = divmod(m, R // 2)
+            st["di", m] = two.tile([P, N], F32, name="di%d" % m, tag="di")
+            nc.vector.tensor_copy(
+                out=st["di", m][:].rearrange("p (c u k) -> p c u k", c=4, u=2),
+                in_=adj_w[g][:, k * N : (k + 1) * N].rearrange("p (c k u) -> p c u k", c=4, u=2),
+            )
 
         def a_(n):
             m, h = divmod(n, 2)
@@ -220,7 +229,7 @@ def tile_msamodel_pa_kernel(tc, x, adj, w, b, out):
             nc.vector.tensor_tensor(out=z[:], in0=st["p2", n][:], in1=bb[:], op=ALU.add)
 
         def c2_on_v(n):
-            return n % 6 == 1
+            return n % 2 == 1 and n >= NU - 8
 
         def c2(n):
             m, h = divmod(n, 2)
@@ -260,6 +269,9 @@ def tile_msamodel_pa_kernel(tc, x, adj, w, b, out):
         def pair(m):
             return [2 * m, 2 * m + 1] if 0 <= m < NPAIR else []
 
+        def deint(m):
+            return m % 2 == 1 and m > 1
+
         xr2(0, 0)
         xr2(0, 1)
         xq(0, 0, 1)
@@ -267,7 +279,8 @@ def tile_msamodel_pa_kernel(tc, x, adj, w, b, out):
         for m in range(2):
             for n in pair(m):
                 t_(n)
-                a_(n)
+                if m == 0:
+                    a_(n)
         qa(0, 0, 1)
         qa(0, 1, 2)
 
@@ -275,25 +288,31 @@ def tile_msamodel_pa_kernel(tc, x, adj, w, b, out):
             g, q = divmod(s, 4)
             more = g + 1 < G
             last = s == NPAIR - 1
-            done = [s - 2]
             for n in pair(s)[0:1]:
                 m1(n)
-            if s == 0:
-                for n in pair(0):
-                    dn(n)
-            if s > 0:
-                for n in pair(s + 2):
-                    a_(n)
-            else:
-                qa(1)
             for n in pair(s + 1):
-                dn(n)
+                a_(n)
+            for n in pair(s):
+                if not last:
+                    dn(n)
             for n in pair(s)[1:2]:
                 m1(n)
-            if 0 <= s - 1 < NPAIR:
+            if 0 <= s - 1 < NPAIR - 2:
                 qb(s - 1)
             for n in pair(s - 2):
-                c1(n)
+                if s != NPAIR:
+                    c1(n)
+            if s - 1 == NPAIR - 2:
+                qb(s - 1)
+            if s == NPAIR:
+                qb(s - 1, 0, 1)
+                c1(2 * (s - 2))
+                qb(s - 1, 1, 2)
+                c1(2 * (s - 2) + 1)
+            if more and q == 3:
+                xr(g + 1, 3, "v")
+            if s + 1 < NPAIR:
+                qa(s + 1)
             for n in pair(s)[0:1]:
                 b_(n)
             for n in pair(s - 1)[0:1]:
@@ -301,12 +320,12 @@ def tile_msamodel_pa_kernel(tc, x, adj, w, b, out):
             if s == 0:
                 st["pb"] = ps_p2.tile([P, D], F32, name="pb", tag="p2")
                 nc.tensor.matmul(out=st["pb"][:], lhsT=ones[:], rhs=zb[:], start=True, stop=True)
-                for n in pair(2):
-                    t_(n)
-                for n in pair(2):
-                    a_(n)
-            for n in pair(s + 3):
+            for n in pair(s + 2):
                 t_(n)
+            if last:
+                for n in pair(s)[1:2]:
+                    b_(n)
+                rb(s // 2)
             for n in pair(s - 2)[0:1]:
                 if not c2_on_v(n):
                     c2(n)
@@ -314,15 +333,19 @@ def tile_msamodel_pa_kernel(tc, x, adj, w, b, out):
                 regroup(wg[:], w_sb[:])
             for n in pair(s - 1)[1:2]:
                 m2(n)
-            if more and (q == 3 or g > 0):
+            if s == NPAIR - 2:
+                for n in pair(s + 1):
+                    dn(n)
+            if more and g > 0 and q < 3:
                 xr(g + 1, q, "v")
             if more and g == 0 and q == 1:
                 xr(1, 0, "v")
             if more and g == 0 and q == 2:
                 xr(1, 1, "v")
                 xr(1, 2, "v")
-            for n in pair(s)[1:2]:
-                b_(n, last)
+            if not last:
+                for n in pair(s)[1:2]:
+                    b_(n)
             if s == 0:
                 nc.scalar.copy(out=bb[:], in_=st["pb"][:])
             for n in pair(s - 2)[1:2]:
@@ -331,13 +354,16 @@ def tile_msamodel_pa_kernel(tc, x, adj, w, b, out):
             for n in pair(s - 2):
                 if c2_on_v(n):
                     c2(n)
-            if 0 <= s - 2:
+            if 0 <= s - 2 < NPAIR - 1:
                 store(s - 2, 0, 2)
-            if s + 2 < NPAIR:
-                qa(s + 2)
+            if s - 2 == NPAIR - 1:
+                store(s - 2, 0, 1)
+                store(s - 2, 1, 2)
+            if s + 3 < NPAIR and deint(s + 3):
+                di(s + 3)
             if more and q == 3:
                 xq(g + 1, 0, 2)
-            if s % 2 == 0 and s < NPAIR:
+            if s % 2 == 1 and s < NPAIR - 1:
                 rb(s // 2)
             if s == 0:
                 nc.vector.quantize_mx(out=wc[:].bitcast(FP8X4), scales=ws[:], in_=wg[:])

@@ -39,6 +39,7 @@ def tile_msamodel_pa_kernel(tc, x, adj, w, b, out):
 
         adj_v = adj.rearrange("g (p r) j -> g p (r j)", r=R)
         x_v = x.rearrange("g (c p t) d -> g p c (t d)", c=2, p=P, t=4)
+        w_v = w.rearrange("(q t i) e -> i q t e", t=4, i=4)
         out_v = out.rearrange("g (p r) e -> g p (r e)", r=R)
 
         adj_sb = [const.tile([P, R * N], BF16, name="adj%d" % g) for g in range(G)]
@@ -65,6 +66,10 @@ def tile_msamodel_pa_kernel(tc, x, adj, w, b, out):
                 in_=x_v[g, :, c0:c1, :],
             )
 
+        def load_w():
+            for i in range(4):
+                nc.sync.dma_start(out=w_sb[i:P:4, :].rearrange("p (t e) -> p t e", t=4), in_=w_v[i, :, :, :])
+
         nc.vector.memset(zb[:], 0.0)
         load_x(0, 0, 1)
         load_x(0, 1, 2)
@@ -73,10 +78,10 @@ def tile_msamodel_pa_kernel(tc, x, adj, w, b, out):
         nc.sync.dma_start(out=zb[0:1, :], in_=b.rearrange("(o n) -> o n", o=1))
         load_adj(0, 2, 4)
         load_adj(0, 4, 6)
-        nc.sync.dma_start(out=w_sb[:], in_=w.rearrange("(p t) e -> p (t e)", t=4))
+        load_w()
         load_adj(0, 6, 8)
-        load_adj(1, 0, 2)
         load_x(1, 0, 1)
+        load_adj(1, 0, 2)
         load_x(1, 1, 2)
         load_adj(1, 2, 4)
         load_adj(1, 4, 8)
@@ -96,25 +101,14 @@ def tile_msamodel_pa_kernel(tc, x, adj, w, b, out):
                 in_=src.rearrange("p (t c i) -> p c t i", t=4, i=4),
             )
 
-        def xr(g, h, eng):
+        def xr(g, h):
             if ("xg", g) not in st:
                 st["xg", g] = two.tile([P, 4 * N], BF16, name="xg%d" % g, tag="xg", align_bytes=64)
             c, v = divmod(h, 2)
             cols = slice(c * 2048, (c + 1) * 2048)
-            dst = st["xg", g][:, cols].rearrange("p (t m j) -> p m j t", t=4, j=4)[:, v * 64 : (v + 1) * 64, :, :]
-            src = x_sb[g][:, cols].rearrange("p (j m t) -> p m j t", t=4, j=4)[:, v * 64 : (v + 1) * 64, :, :]
-            if eng == "s":
-                nc.scalar.copy(out=dst, in_=src)
-            else:
-                nc.vector.tensor_copy(out=dst, in_=src)
-
-        def xr2(g, c):
-            if ("xg", g) not in st:
-                st["xg", g] = two.tile([P, 4 * N], BF16, name="xg%d" % g, tag="xg", align_bytes=64)
-            nc.vector.tensor_copy(
-                out=st["xg", g][:, c * 2048 : (c + 1) * 2048].rearrange("p (t m j) -> p m j t", t=4, j=4),
-                in_=x_sb[g][:, c * 2048 : (c + 1) * 2048].rearrange("p (j m t) -> p m j t", t=4, j=4),
-            )
+            dst = st["xg", g][:, cols].rearrange("p (t q i j) -> p q t j i", t=4, i=4, j=4)
+            src = x_sb[g][:, cols].rearrange("p (j q t i) -> p q t j i", j=4, t=4, i=4)
+            nc.vector.tensor_copy(out=dst[:, 16 * v : 16 * v + 16, :, :, :], in_=src[:, 16 * v : 16 * v + 16, :, :, :])
 
         def xq(g, c0, c1):
             if c0 == 0:
@@ -270,10 +264,12 @@ def tile_msamodel_pa_kernel(tc, x, adj, w, b, out):
             return [2 * m, 2 * m + 1] if 0 <= m < NPAIR else []
 
         def deint(m):
-            return m % 2 == 1 and m > 1
+            return (m % 2 == 1 and m > 1) or m == NPAIR - 2
 
-        xr2(0, 0)
-        xr2(0, 1)
+        xr(0, 0)
+        xr(0, 1)
+        xr(0, 2)
+        xr(0, 3)
         xq(0, 0, 1)
         xq(0, 1, 2)
         for m in range(2):
@@ -310,7 +306,7 @@ def tile_msamodel_pa_kernel(tc, x, adj, w, b, out):
                 qb(s - 1, 1, 2)
                 c1(2 * (s - 2) + 1)
             if more and q == 3:
-                xr(g + 1, 3, "v")
+                xr(g + 1, 3)
             if s + 1 < NPAIR:
                 qa(s + 1)
             for n in pair(s)[0:1]:
@@ -336,13 +332,14 @@ def tile_msamodel_pa_kernel(tc, x, adj, w, b, out):
             if s == NPAIR - 2:
                 for n in pair(s + 1):
                     dn(n)
-            if more and g > 0 and q < 3:
-                xr(g + 1, q, "v")
-            if more and g == 0 and q == 1:
-                xr(1, 0, "v")
-            if more and g == 0 and q == 2:
-                xr(1, 1, "v")
-                xr(1, 2, "v")
+            if more and q == (1 if g == 0 else 0):
+                xr(g + 1, 0)
+            if more and q == 1:
+                xr(g + 1, 1)
+            if more and q == (2 if g == 0 else 1):
+                xr(g + 1, 2)
+            if more and q == 2:
+                xq(g + 1, 0, 1)
             if not last:
                 for n in pair(s)[1:2]:
                     b_(n)
@@ -362,7 +359,7 @@ def tile_msamodel_pa_kernel(tc, x, adj, w, b, out):
             if s + 3 < NPAIR and deint(s + 3):
                 di(s + 3)
             if more and q == 3:
-                xq(g + 1, 0, 2)
+                xq(g + 1, 1, 2)
             if s % 2 == 1 and s < NPAIR - 1:
                 rb(s // 2)
             if s == 0:

@@ -101,14 +101,16 @@ def tile_msamodel_pa_kernel(tc, x, adj, w, b, out):
                 in_=src.rearrange("p (t c i) -> p c t i", t=4, i=4),
             )
 
-        def xr(g, h):
+        def xr(g, c, q0, q1):
             if ("xg", g) not in st:
                 st["xg", g] = two.tile([P, 4 * N], BF16, name="xg%d" % g, tag="xg", align_bytes=64)
-            c, v = divmod(h, 2)
             cols = slice(c * 2048, (c + 1) * 2048)
             dst = st["xg", g][:, cols].rearrange("p (t q i j) -> p q t j i", t=4, i=4, j=4)
             src = x_sb[g][:, cols].rearrange("p (j q t i) -> p q t j i", j=4, t=4, i=4)
-            nc.vector.tensor_copy(out=dst[:, 16 * v : 16 * v + 16, :, :, :], in_=src[:, 16 * v : 16 * v + 16, :, :, :])
+            nc.vector.tensor_copy(out=dst[:, q0:q1, :, :, :], in_=src[:, q0:q1, :, :, :])
+
+        def xh(g, h):
+            xr(g, h // 2, 16 * (h % 2), 16 * (h % 2) + 16)
 
         def xq(g, c0, c1):
             if c0 == 0:
@@ -217,32 +219,32 @@ def tile_msamodel_pa_kernel(tc, x, adj, w, b, out):
                 stop=True,
             )
 
-        def c1(n):
-            z = zs.tile([P, D], F32, name="z%d" % n, tag="z")
-            st["z", n] = z
-            nc.vector.tensor_tensor(out=z[:], in0=st["p2", n][:], in1=bb[:], op=ALU.add)
+        def c1(n, e0=0, e1=D):
+            if e0 == 0:
+                st["z", n] = zs.tile([P, D], F32, name="z%d" % n, tag="z")
+            nc.vector.tensor_tensor(
+                out=st["z", n][:, e0:e1], in0=st["p2", n][:, e0:e1], in1=bb[:, e0:e1], op=ALU.add
+            )
 
         def c2_on_v(n):
-            return n % 2 == 1 and n >= NU - 8
+            return n in (NU - 7, NU - 5)
 
-        def c2(n):
+        def c2(n, e0=0, e1=D):
             m, h = divmod(n, 2)
             if ("o", m) not in st:
                 st["o", m] = five.tile([P, 2 * D], F32, name="o%d" % m, tag="o")
-            o = st["o", m][:, h * D : (h + 1) * D]
+            o = st["o", m][:, h * D + e0 : h * D + e1]
             rd = r_t[n // 4][:, n % 4 : n % 4 + 1]
             if c2_on_v(n):
                 nc.vector.tensor_scalar(
-                    out=o, in0=st["z", n][:], scalar1=rd, scalar2=0.0, op0=ALU.mult, op1=ALU.max
+                    out=o, in0=st["z", n][:, e0:e1], scalar1=rd, scalar2=0.0, op0=ALU.mult, op1=ALU.max
                 )
             else:
-                nc.scalar.activation(out=o, in_=st["z", n][:], func=ACT.Relu, scale=rd)
+                nc.scalar.activation(out=o, in_=st["z", n][:, e0:e1], func=ACT.Relu, scale=rd)
 
-        def store(m, u0, u1):
+        def store(m, e0=0, e1=2 * D):
             g, k = divmod(m, R // 2)
-            nc.sync.dma_start(
-                out=out_v[g, :, (2 * k + u0) * D : (2 * k + u1) * D], in_=st["o", m][:, u0 * D : u1 * D]
-            )
+            nc.sync.dma_start(out=out_v[g, :, 2 * k * D + e0 : 2 * k * D + e1], in_=st["o", m][:, e0:e1])
 
         def dn(n):
             m, h = divmod(n, 2)
@@ -256,8 +258,10 @@ def tile_msamodel_pa_kernel(tc, x, adj, w, b, out):
                     stop=(k == 7),
                 )
 
-        def rb(k):
+        def re(k):
             nc.vector.tensor_scalar_add(out=e_t[k][:], in0=pd[:, 4 * k : 4 * k + 4], scalar1=1.0)
+
+        def rr(k):
             nc.vector.reciprocal(out=r_t[k][:], in_=e_t[k][:])
 
         def pair(m):
@@ -266,10 +270,8 @@ def tile_msamodel_pa_kernel(tc, x, adj, w, b, out):
         def deint(m):
             return (m % 2 == 1 and m > 1) or m == NPAIR - 2
 
-        xr(0, 0)
-        xr(0, 1)
-        xr(0, 2)
-        xr(0, 3)
+        xr(0, 0, 0, 32)
+        xr(0, 1, 0, 32)
         xq(0, 0, 1)
         xq(0, 1, 2)
         for m in range(2):
@@ -280,7 +282,7 @@ def tile_msamodel_pa_kernel(tc, x, adj, w, b, out):
         qa(0, 0, 1)
         qa(0, 1, 2)
 
-        for s in range(NPAIR + 2):
+        for s in range(NPAIR + 1):
             g, q = divmod(s, 4)
             more = g + 1 < G
             last = s == NPAIR - 1
@@ -296,7 +298,7 @@ def tile_msamodel_pa_kernel(tc, x, adj, w, b, out):
             if 0 <= s - 1 < NPAIR - 2:
                 qb(s - 1)
             for n in pair(s - 2):
-                if s != NPAIR:
+                if s < NPAIR:
                     c1(n)
             if s - 1 == NPAIR - 2:
                 qb(s - 1)
@@ -306,9 +308,14 @@ def tile_msamodel_pa_kernel(tc, x, adj, w, b, out):
                 qb(s - 1, 1, 2)
                 c1(2 * (s - 2) + 1)
             if more and q == 3:
-                xr(g + 1, 3)
+                xh(g + 1, 3)
             if s + 1 < NPAIR:
                 qa(s + 1)
+            if s % 2 == 1 and s < NPAIR - 1:
+                re(s // 2)
+            for n in pair(s - 2)[0:1]:
+                if not c2_on_v(n):
+                    c2(n)
             for n in pair(s)[0:1]:
                 b_(n)
             for n in pair(s - 1)[0:1]:
@@ -321,10 +328,8 @@ def tile_msamodel_pa_kernel(tc, x, adj, w, b, out):
             if last:
                 for n in pair(s)[1:2]:
                     b_(n)
-                rb(s // 2)
-            for n in pair(s - 2)[0:1]:
-                if not c2_on_v(n):
-                    c2(n)
+                re(s // 2)
+                rr(s // 2)
             if s == 0:
                 regroup(wg[:], w_sb[:])
             for n in pair(s - 1)[1:2]:
@@ -333,11 +338,11 @@ def tile_msamodel_pa_kernel(tc, x, adj, w, b, out):
                 for n in pair(s + 1):
                     dn(n)
             if more and q == (1 if g == 0 else 0):
-                xr(g + 1, 0)
+                xh(g + 1, 0)
             if more and q == 1:
-                xr(g + 1, 1)
+                xh(g + 1, 1)
             if more and q == (2 if g == 0 else 1):
-                xr(g + 1, 2)
+                xh(g + 1, 2)
             if more and q == 2:
                 xq(g + 1, 0, 1)
             if not last:
@@ -351,16 +356,27 @@ def tile_msamodel_pa_kernel(tc, x, adj, w, b, out):
             for n in pair(s - 2):
                 if c2_on_v(n):
                     c2(n)
-            if 0 <= s - 2 < NPAIR - 1:
-                store(s - 2, 0, 2)
-            if s - 2 == NPAIR - 1:
-                store(s - 2, 0, 1)
-                store(s - 2, 1, 2)
-            if s + 3 < NPAIR and deint(s + 3):
-                di(s + 3)
+            if 0 <= s - 2 < NPAIR - 2:
+                store(s - 2)
+            elif s - 2 >= NPAIR - 2:
+                store(s - 2, 0, D)
+                store(s - 2, D, 2 * D)
             if more and q == 3:
                 xq(g + 1, 1, 2)
+            if s + 3 < NPAIR and deint(s + 3):
+                di(s + 3)
             if s % 2 == 1 and s < NPAIR - 1:
-                rb(s // 2)
+                rr(s // 2)
             if s == 0:
                 nc.vector.quantize_mx(out=wc[:].bitcast(FP8X4), scales=ws[:], in_=wg[:])
+
+        m = NPAIR - 1
+        c1(2 * m)
+        c1(2 * m + 1, 0, D // 2)
+        c2(2 * m)
+        store(m, 0, D)
+        c1(2 * m + 1, D // 2, D)
+        c2(2 * m + 1, 0, D // 2)
+        store(m, D, D + D // 2)
+        c2(2 * m + 1, D // 2, D)
+        store(m, D + D // 2, 2 * D)

from contextlib import ExitStack

import concourse.mybir as mybir
from concourse.masks import make_identity

F32 = mybir.dt.float32
BF16 = mybir.dt.bfloat16
U32 = mybir.dt.uint32
U8 = mybir.dt.uint8
FP8X4 = mybir.dt.float8_e4m3fn_x4
ALU = mybir.AluOpType
ACT = mybir.ActivationFunctionType

G = 4
N = 1024
D = 512
P = 128
R = N // P
NU = G * R
NPAIR = NU // 2
FLOPS = 2 * G * N * N * D + 2 * G * N * D * D


def tile_msamodel_pa_kernel(tc, x, adj, w, b, out):
    nc = tc.nc
    with ExitStack() as ctx:
        const = ctx.enter_context(tc.tile_pool(name="const", bufs=1))
        two = ctx.enter_context(tc.tile_pool(name="two", bufs=2))
        three = ctx.enter_context(tc.tile_pool(name="three", bufs=3))
        four = ctx.enter_context(tc.tile_pool(name="four", bufs=4))
        five = ctx.enter_context(tc.tile_pool(name="five", bufs=5))
        gts = ctx.enter_context(tc.tile_pool(name="gts", bufs=6))
        zs = ctx.enter_context(tc.tile_pool(name="zs", bufs=5))
        ps_tp = ctx.enter_context(tc.psum_pool(name="ps_tp", bufs=2))
        ps_p1 = ctx.enter_context(tc.psum_pool(name="ps_p1", bufs=3))
        ps_p2 = ctx.enter_context(tc.psum_pool(name="ps_p2", bufs=2))
        ps_pd = ctx.enter_context(tc.psum_pool(name="ps_pd", bufs=1))
        ctx.enter_context(tc.manual_schedule())

        adj_v = adj.rearrange("g (p r) j -> g p (r j)", r=R)
        x_v = x.rearrange("g (c p t) d -> g p c (t d)", c=2, p=P, t=4)
        w_v = w.rearrange("(q t i) e -> i q t e", t=4, i=4)
        out_v = out.rearrange("g (p r) e -> g p (r e)", r=R)

        adj_sb = [const.tile([P, R * N], BF16, name="adj%d" % g) for g in range(G)]
        adj_w = [t[:].bitcast(F32) for t in adj_sb]
        x_sb = [const.tile([P, 4 * N], BF16, name="x%d" % g) for g in range(G)]
        w_sb = const.tile([P, 4 * D], BF16, name="w_sb")
        wg = const.tile([P, 4 * D], BF16, name="wg", align_bytes=64)
        wc = const.tile([P, D], U32, name="wc", align_bytes=64)
        ws = const.tile([P, D], U8, name="ws", align_bytes=64)
        zb = const.tile([P, D], BF16, name="zb")
        ones = const.tile([P, P], BF16, name="ones")
        identf = const.tile([P, P], F32, name="identf")
        bb = const.tile([P, D], F32, name="bb")
        e_t = [const.tile([P, 4], F32, name="e_t%d" % k) for k in range(NU // 4)]
        r_t = [const.tile([P, 4], F32, name="r_t%d" % k) for k in range(NU // 4)]
        pd = ps_pd.tile([P, NU], F32, name="pd")

        def load_adj(g, r0, r1):
            nc.sync.dma_start(out=adj_sb[g][:, r0 * N : r1 * N], in_=adj_v[g, :, r0 * N : r1 * N])

        def load_x(g, c0, c1):
            nc.sync.dma_start(
                out=x_sb[g][:, c0 * 2048 : c1 * 2048].rearrange("p (c f) -> p c f", f=2048),
                in_=x_v[g, :, c0:c1, :],
            )

        def load_w():
            for i in range(4):
                nc.sync.dma_start(out=w_sb[i:P:4, :].rearrange("p (t e) -> p t e", t=4), in_=w_v[i, :, :, :])

        nc.vector.memset(zb[:], 0.0)
        load_x(0, 0, 1)
        load_x(0, 1, 2)
        load_adj(0, 0, 1)
        load_adj(0, 1, 2)
        nc.sync.dma_start(out=zb[0:1, :], in_=b.rearrange("(o n) -> o n", o=1))
        load_adj(0, 2, 4)
        load_adj(0, 4, 6)
        load_w()
        load_adj(0, 6, 8)
        load_x(1, 0, 1)
        load_adj(1, 0, 2)
        load_x(1, 1, 2)
        load_adj(1, 2, 4)
        load_adj(1, 4, 8)
        load_x(2, 0, 2)
        load_adj(2, 0, 8)
        load_x(3, 0, 2)
        load_adj(3, 0, 8)

        nc.vector.memset(ones[:], 1.0)
        make_identity(nc, identf[:])

        st = {}

        def regroup(dst, src):
            nc.vector.tensor_copy(
                out=dst.rearrange("p (c i t) -> p c t i", i=4, t=4),
                in_=src.rearrange("p (t c i) -> p c t i", t=4, i=4),
            )

        def xr(g, c, q0, q1):
            if ("xg", g) not in st:
                st["xg", g] = two.tile([P, 4 * N], BF16, name="xg%d" % g, tag="xg", align_bytes=64)
            cols = slice(c * 2048, (c + 1) * 2048)
            dst = st["xg", g][:, cols].rearrange("p (t q i j) -> p q t j i", t=4, i=4, j=4)
            src = x_sb[g][:, cols].rearrange("p (j q t i) -> p q t j i", j=4, t=4, i=4)
            nc.vector.tensor_copy(out=dst[:, q0:q1, :, :, :], in_=src[:, q0:q1, :, :, :])

        def xh(g, h):
            xr(g, h // 2, 16 * (h % 2), 16 * (h % 2) + 16)

        def xq(g, c0, c1):
            if c0 == 0:
                st["xc", g] = two.tile([P, N], U32, name="xc%d" % g, tag="xc", align_bytes=64)
                st["xs", g] = two.tile([P, N], U8, name="xs%d" % g, tag="xs", align_bytes=64)
            nc.vector.quantize_mx(
                out=st["xc", g][:, c0 * D : c1 * D].bitcast(FP8X4),
                scales=st["xs", g][:, c0 * D : c1 * D],
                in_=st["xg", g][:, c0 * 2048 : c1 * 2048],
            )

        def t_(n):
            g, r = divmod(n, R)
            tp = ps_tp.tile([P, 512], F32, name="tp%d" % n, tag="tp")
            st["tp", n] = tp
            for k in range(4):
                if ("di", n // 2) in st:
                    lo = (n % 2) * 512 + k * P
                    words = st["di", n // 2][:, lo : lo + P]
                else:
                    lo = r * 512 + (k // 2) * 256 + k % 2
                    words = adj_w[g][:, lo : lo + 255 : 2]
                nc.tensor.transpose(out=tp[:, k * P : (k + 1) * P], in_=words, identity=identf[:])

        def di(m):
            g, k = divmod(m, R // 2)
            st["di", m] = two.tile([P, N], F32, name="di%d" % m, tag="di")
            nc.vector.tensor_copy(
                out=st["di", m][:].rearrange("p (c u k) -> p c u k", c=4, u=2),
                in_=adj_w[g][:, k * N : (k + 1) * N].rearrange("p (c k u) -> p c u k", c=4, u=2),
            )

        def a_(n):
            m, h = divmod(n, 2)
            if h == 0:
                st["gt", m] = gts.tile([P, 2 * N], BF16, name="gt%d" % m, tag="gt", align_bytes=64)
            nc.scalar.copy(
                out=st["gt", m][:, h * N : (h + 1) * N].bitcast(F32).rearrange("p (c i u) -> p c i u", c=2, u=2),
                in_=st["tp", n][:].rearrange("p (c u i) -> p c i u", c=2, u=2),
            )

        def qa(m, h0=0, h1=2):
            if h0 == 0:
                st["ac", m] = four.tile([P, 512], U32, name="ac%d" % m, tag="ac", align_bytes=64)
                st["as", m] = four.tile([P, 512], U8, name="as%d" % m, tag="as", align_bytes=64)
            nc.vector.quantize_mx(
                out=st["ac", m][:, h0 * 256 : h1 * 256].bitcast(FP8X4),
                scales=st["as", m][:, h0 * 256 : h1 * 256],
                in_=st["gt", m][:, h0 * N : h1 * N],
            )

        def m1(n):
            g = n // R
            m, h = divmod(n, 2)
            p1 = ps_p1.tile([P, 512], F32, name="p1_%d" % n, tag="p1")
            st["p1", n] = p1
            for t in range(4):
                for c in range(2):
                    lo = c * D + t * P
                    ro = (2 * h + c) * P
                    nc.tensor.matmul_mx(
                        out=p1[:, t * P : (t + 1) * P],
                        lhsT=st["xc", g][:, lo : lo + P].bitcast(FP8X4),
                        lhsT_scale=st["xs", g][:, lo : lo + P],
                        rhs=st["ac", m][:, ro : ro + P].bitcast(FP8X4),
                        rhs_scale=st["as", m][:, ro : ro + P],
                        start=(c == 0),
                        stop=(c == 1),
                    )

        def b_(n, on_v=False):
            m, h = divmod(n, 2)
            if h == 0:
                st["g2", m] = three.tile([P, 2 * D], BF16, name="g2_%d" % m, tag="g2", align_bytes=64)
            dst = st["g2", m][:, h * D : (h + 1) * D].rearrange("p (i t) -> p i t", t=4)
            src = st["p1", n][:].rearrange("p (t i) -> p i t", t=4)
            if on_v:
                nc.vector.tensor_copy(out=dst, in_=src)
            else:
                nc.scalar.copy(out=dst, in_=src)

        def qb(m, h0=0, h1=2):
            if h0 == 0:
                st["bc", m] = three.tile([P, 2 * P], U32, name="bc%d" % m, tag="bc", align_bytes=64)
                st["bs", m] = three.tile([P, 2 * P], U8, name="bs%d" % m, tag="bs", align_bytes=64)
            nc.vector.quantize_mx(
                out=st["bc", m][:, h0 * P : h1 * P].bitcast(FP8X4),
                scales=st["bs", m][:, h0 * P : h1 * P],
                in_=st["g2", m][:, h0 * D : h1 * D],
            )

        def m2(n):
            m, h = divmod(n, 2)
            if m in (NPAIR - 3, NPAIR - 1):
                p2 = ps_tp.tile([P, D], F32, name="p2_%d" % n, tag="tp")
            else:
                p2 = ps_p2.tile([P, D], F32, name="p2_%d" % n, tag="p2")
            st["p2", n] = p2
            nc.tensor.matmul_mx(
                out=p2[:],
                lhsT=st["bc", m][:, h * P : (h + 1) * P].bitcast(FP8X4),
                lhsT_scale=st["bs", m][:, h * P : (h + 1) * P],
                rhs=wc[:].bitcast(FP8X4),
                rhs_scale=ws[:],
                start=True,
                stop=True,
            )

        def c1(n, e0=0, e1=D):
            if e0 == 0:
                st["z", n] = zs.tile([P, D], F32, name="z%d" % n, tag="z")
            nc.vector.tensor_tensor(
                out=st["z", n][:, e0:e1], in0=st["p2", n][:, e0:e1], in1=bb[:, e0:e1], op=ALU.add
            )

        def c2_on_v(n):
            return n in (NU - 7, NU - 5)

        def c2(n, e0=0, e1=D):
            m, h = divmod(n, 2)
            if ("o", m) not in st:
                st["o", m] = five.tile([P, 2 * D], F32, name="o%d" % m, tag="o")
            o = st["o", m][:, h * D + e0 : h * D + e1]
            rd = r_t[n // 4][:, n % 4 : n % 4 + 1]
            if c2_on_v(n):
                nc.vector.tensor_scalar(
                    out=o, in0=st["z", n][:, e0:e1], scalar1=rd, scalar2=0.0, op0=ALU.mult, op1=ALU.max
                )
            else:
                nc.scalar.activation(out=o, in_=st["z", n][:, e0:e1], func=ACT.Relu, scale=rd)

        def store(m, e0=0, e1=2 * D):
            g, k = divmod(m, R // 2)
            nc.sync.dma_start(out=out_v[g, :, 2 * k * D + e0 : 2 * k * D + e1], in_=st["o", m][:, e0:e1])

        def dn(n):
            m, h = divmod(n, 2)
            cols = st["gt", m][:, h * N : (h + 1) * N].rearrange("p (c i t) -> p c t i", c=2, t=4)
            for k in range(8):
                nc.tensor.matmul(
                    out=pd[:, n : n + 1],
                    lhsT=cols[:, k // 4, k % 4, :],
                    rhs=ones[:, 0:1],
                    start=(k == 0),
                    stop=(k == 7),
                )

        def re(k):
            nc.vector.tensor_scalar_add(out=e_t[k][:], in0=pd[:, 4 * k : 4 * k + 4], scalar1=1.0)

        def rr(k):
            nc.vector.reciprocal(out=r_t[k][:], in_=e_t[k][:])

        def pair(m):
            return [2 * m, 2 * m + 1] if 0 <= m < NPAIR else []

        def deint(m):
            return (m % 2 == 1 and m > 1) or m == NPAIR - 2

        xr(0, 0, 0, 32)
        xr(0, 1, 0, 32)
        xq(0, 0, 1)
        xq(0, 1, 2)
        for m in range(2):
            for n in pair(m):
                t_(n)
                if m == 0:
                    a_(n)
        qa(0, 0, 1)
        qa(0, 1, 2)

        for s in range(NPAIR + 1):
            g, q = divmod(s, 4)
            more = g + 1 < G
            last = s == NPAIR - 1
            for n in pair(s)[0:1]:
                m1(n)
            for n in pair(s + 1):
                a_(n)
            for n in pair(s):
                if not last:
                    dn(n)
            for n in pair(s)[1:2]:
                m1(n)
            if 0 <= s - 1 < NPAIR - 2:
                qb(s - 1)
            for n in pair(s - 2):
                if s < NPAIR:
                    c1(n)
            if s - 1 == NPAIR - 2:
                qb(s - 1)
            if s == NPAIR:
                qb(s - 1, 0, 1)
                c1(2 * (s - 2))
                qb(s - 1, 1, 2)
                c1(2 * (s - 2) + 1)
            if more and q == 3:
                xh(g + 1, 3)
            if s + 1 < NPAIR:
                qa(s + 1)
            if s % 2 == 1 and s < NPAIR - 1:
                re(s // 2)
            for n in pair(s - 2)[0:1]:
                if not c2_on_v(n):
                    c2(n)
            for n in pair(s)[0:1]:
                b_(n)
            for n in pair(s - 1)[0:1]:
                m2(n)
            if s == 0:
                st["pb"] = ps_p2.tile([P, D], F32, name="pb", tag="p2")
                nc.tensor.matmul(out=st["pb"][:], lhsT=ones[:], rhs=zb[:], start=True, stop=True)
            for n in pair(s + 2):
                t_(n)
            if last:
                for n in pair(s)[1:2]:
                    b_(n)
                re(s // 2)
                rr(s // 2)
            if s == 0:
                regroup(wg[:], w_sb[:])
            for n in pair(s - 1)[1:2]:
                m2(n)
            if s == NPAIR - 2:
                for n in pair(s + 1):
                    dn(n)
            if more and q == (1 if g == 0 else 0):
                xh(g + 1, 0)
            if more and q == 1:
                xh(g + 1, 1)
            if more and q == (2 if g == 0 else 1):
                xh(g + 1, 2)
            if more and q == 2:
                xq(g + 1, 0, 1)
            if not last:
                for n in pair(s)[1:2]:
                    b_(n)
            if s == 0:
                nc.scalar.copy(out=bb[:], in_=st["pb"][:])
            for n in pair(s - 2)[1:2]:
                if not c2_on_v(n):
                    c2(n)
            for n in pair(s - 2):
                if c2_on_v(n):
                    c2(n)
            if 0 <= s - 2 < NPAIR - 2:
                store(s - 2)
            elif s - 2 >= NPAIR - 2:
                store(s - 2, 0, D)
                store(s - 2, D, 2 * D)
            if more and q == 3:
                xq(g + 1, 1, 2)
            if s + 3 < NPAIR and deint(s + 3):
                di(s + 3)
            if s % 2 == 1 and s < NPAIR - 1:
                rr(s // 2)
            if s == 0:
                nc.vector.quantize_mx(out=wc[:].bitcast(FP8X4), scales=ws[:], in_=wg[:])

        m = NPAIR - 1
        c1(2 * m)
        c1(2 * m + 1, 0, D // 2)
        c2(2 * m)
        store(m, 0, D)
        c1(2 * m + 1, D // 2, D)
        c2(2 * m + 1, 0, D // 2)
        store(m, D, D + D // 2)
        c2(2 * m + 1, D // 2, D)
        store(m, D + D // 2, 2 * D)
